import numpy as np
import ml_dtypes


def mxq(x, axis, fmt="e4m3"):
    dtype, down = {"e4m3": (ml_dtypes.float8_e4m3fn, 7), "e5m2": (ml_dtypes.float8_e5m2, 14)}[fmt]
    v = np.moveaxis(np.asarray(x, np.float32).astype(ml_dtypes.bfloat16).astype(np.float64), axis, -1)
    blocks = v.reshape(v.shape[:-1] + (-1, 32))
    amax = np.abs(blocks).max(-1, keepdims=True)
    byte = np.maximum(np.where(amax > 0, np.frexp(amax)[1] - 1 + 127, 0) - down, 1)
    scale = np.exp2(byte - 127.0)
    codes = (blocks / scale).astype(np.float32).astype(dtype).astype(np.float64)
    return np.moveaxis((codes * scale).reshape(v.shape), -1, axis)


WIDE = False


def mx_kscale(k):
    if not WIDE:
        return np.ones(k)
    levels = np.array([10, -10, 5, -5, 0])
    a = np.random.permutation(np.resize(levels, k // 512 * 4)).reshape(k // 512, 4)
    idx = np.arange(k)
    return np.exp2(a[idx // 512, idx % 128 // 32])


BF16 = ml_dtypes.bfloat16


def bf(x):
    return np.asarray(x, np.float32).astype(BF16)


def f64(x):
    return np.asarray(x).astype(np.float64)


E2M1 = np.array([0.0, 0.5, 1.0, 1.5, 2.0, 3.0, 4.0, 6.0, -0.0, -0.5, -1.0, -1.5, -2.0, -3.0, -4.0, -6.0])


def pack_weight(w, fmt):
    k, n = w.shape
    w = f64(bf(w)).reshape(k // 32, 32, n)
    amax = np.abs(w).max(1)
    if fmt == "e4m3":
        byte = np.frexp(amax)[1] - 1 + 127 - 7
    else:
        mant, ex = np.frexp(amax / 6.0)
        byte = np.where(mant > 0.5, ex, ex - 1) + 127
    byte = np.clip(np.where(amax > 0, byte, 1), 1, 254)
    scaled = (w * np.exp2(127.0 - byte)[:, None, :]).reshape(k, n).astype(np.float32)
    by_word = np.ascontiguousarray(scaled.reshape(k // 512, 128, 4, n).transpose(0, 1, 3, 2))
    if fmt == "e4m3":
        words = by_word.astype(ml_dtypes.float8_e4m3fn).view(np.uint8)
    else:
        c = by_word.astype(ml_dtypes.float4_e2m1fn).view(np.uint8) & 0xF
        words = c[..., 0::2] | (c[..., 1::2] << 4)
    return np.ascontiguousarray(words), np.ascontiguousarray(byte.astype(np.uint8).reshape(k // 512, 16, n))


def unpack_weight(words, scales, fmt):
    g, p, n, _ = words.shape
    if fmt == "e4m3":
        vals = np.ascontiguousarray(words).view(ml_dtypes.float8_e4m3fn).astype(np.float64)
    else:
        nib = np.empty((g, p, n, 4), np.uint8)
        nib[..., 0::2] = words & 0xF
        nib[..., 1::2] = words >> 4
        vals = E2M1[nib]
    vals = vals * np.repeat(np.exp2(scales.astype(np.float64) - 127.0), 8, axis=1)[..., None]
    return vals.transpose(0, 1, 3, 2).reshape(g * 512, n)


B, C, H, W = 2, 512, 64, 64
N = H * W
KV = 0.05 * N / np.sqrt(C)
FMT = "e4m3"


def setup_inputs():
    s, t = mx_kscale(C), mx_kscale(C)
    x = bf(np.random.standard_normal((B, C, H, W)) * s[None, :, None, None])
    mask = bf(np.random.random_sample((B, 1, H, W)))
    W_q_words, W_q_scales = pack_weight(np.random.standard_normal((C, C)) / np.sqrt(C) / s[:, None], FMT)
    b_q = bf(np.random.standard_normal(C) * 0.3)
    kv_know = bf(np.random.standard_normal((B, 1, C)) * KV * t)
    kv_mask = bf(np.random.standard_normal((B, 1, C)) * KV * t)
    W_out_words, W_out_scales = pack_weight(np.random.standard_normal((C, C)) / KV / t[:, None], FMT)
    b_out = bf(np.random.standard_normal(C) * 0.2)
    return {"x": x,
            "mask": mask,
            "W_q_words": W_q_words,
            "W_q_scales": W_q_scales,
            "b_q": b_q,
            "kv_know": kv_know,
            "kv_mask": kv_mask,
            "W_out_words": W_out_words,
            "W_out_scales": W_out_scales,
            "b_out": b_out}


def reference(x, mask, W_q_words, W_q_scales, b_q, kv_know, kv_mask, W_out_words, W_out_scales, b_out):
    x, mask = f64(x), f64(mask)
    b, c, h, w = x.shape
    xf = np.transpose(x, (0, 2, 3, 1)).reshape(b, h * w, c)
    q = (mxq(xf, 2, "e4m3") @ unpack_weight(W_q_words, W_q_scales, FMT)) + f64(b_q)
    q = q / np.linalg.norm(q, axis=-1, keepdims=True)
    m = np.transpose(mask, (0, 2, 3, 1)).reshape(b, h * w, 1)
    inv = 1.0 - m
    qu = q * inv
    qm = q * m
    out_know = f64(kv_know) * qu
    out_mask = f64(kv_mask) * qm
    out = out_know * inv + m * (0.3 * out_know + 0.7 * out_mask)
    return (mxq(out, 2, "e4m3") @ unpack_weight(W_out_words, W_out_scales, FMT)) + f64(b_out)

@@ -1,0 +1,224 @@
+from contextlib import ExitStack
+
+import concourse.mybir as mybir
+from concourse.masks import make_identity
+
+F32 = mybir.dt.float32
+BF16 = mybir.dt.bfloat16
+I32 = mybir.dt.int32
+U32 = mybir.dt.uint32
+U8 = mybir.dt.uint8
+FP8X4 = mybir.dt.float8_e4m3fn_x4
+ALU = mybir.AluOpType
+ACT = mybir.ActivationFunctionType
+
+P = 128
+PACK = 4
+IMAGES = 2
+C = 512
+PIXELS = 4096
+GROUP = 512
+TILES = GROUP // P
+BLOCKS = C // P
+GROUPS_PER_IMAGE = PIXELS // GROUP
+GROUPS = IMAGES * GROUPS_PER_IMAGE
+CHUNK = 1024
+GROUPS_PER_CHUNK = CHUNK // GROUP
+RUN = 4
+
+FLOPS = 2 * 2 * IMAGES * PIXELS * C * C
+
+
+def load_weight(nc, pool, words, scales, label):
+    codes = pool.tile([P, C], U32, name=label + "_codes", align_bytes=64)
+    plane = pool.tile([P, C], U8, name=label + "_plane", align_bytes=64)
+    nc.vector.memset(plane[:].bitcast(I32), 0)
+    nc.sync.dma_start(out=codes[:].bitcast(I32), in_=words[0].rearrange("p n t -> p (n t)").bitcast(I32))
+    for quadrant in range(4):
+        nc.sync.dma_start(
+            out=plane[32 * quadrant : 32 * quadrant + 4, :].bitcast(I32),
+            in_=scales[0, 4 * quadrant : 4 * quadrant + 4, :].bitcast(I32),
+        )
+    return codes, plane
+
+
+def tile_hydraattention_pb_t_kernel(
+    tc, x, mask, W_q_words, W_q_scales, b_q, kv_know, kv_mask, W_out_words, W_out_scales, b_out, out
+):
+    nc = tc.nc
+    with ExitStack() as stack:
+        const = stack.enter_context(tc.tile_pool(name="const", bufs=1))
+        x_pool = stack.enter_context(tc.tile_pool(name="x_pool", bufs=IMAGES * PIXELS // CHUNK))
+        work = stack.enter_context(tc.tile_pool(name="work", bufs=2))
+        tiles3 = stack.enter_context(tc.tile_pool(name="tiles3", bufs=3))
+        small = stack.enter_context(tc.tile_pool(name="small", bufs=4))
+        psum_q = stack.enter_context(tc.psum_pool(name="psum_q", bufs=2))
+        psum_t = stack.enter_context(tc.psum_pool(name="psum_t", bufs=3))
+        psum_g = stack.enter_context(tc.psum_pool(name="psum_g", bufs=1))
+        psum_y = stack.enter_context(tc.psum_pool(name="psum_y", bufs=2))
+
+        x_raw = []
+        for chunk in range(IMAGES * PIXELS // CHUNK):
+            image, part = divmod(chunk, PIXELS // CHUNK)
+            raw = x_pool.tile([P, PACK, CHUNK], BF16, name="x_raw")
+            x_raw.append(raw)
+            rows = x[image].rearrange("(p t) h w -> p t (h w)", t=PACK)
+            nc.sync.dma_start(out=raw[:], in_=rows[:, :, part * CHUNK : (part + 1) * CHUNK])
+            if chunk == 0:
+                wq_codes, wq_plane = load_weight(nc, const, W_q_words, W_q_scales, "wq")
+                rows_in = const.tile([P, P], BF16, name="rows_in")
+                nc.vector.memset(rows_in[:], 0.0)
+                nc.sync.dma_start(out=rows_in[0:64, :], in_=mask.rearrange("b o (r a) w -> (b o r) (a w)", a=2))
+                nc.sync.dma_start(out=rows_in[64:68, :], in_=b_q.rearrange("(j m) -> j m", m=P))
+                wo_codes, wo_plane = load_weight(nc, const, W_out_words, W_out_scales, "wo")
+
+        know_rows, mask_rows = [], []
+        for image in range(IMAGES):
+            kk = const.tile([P, C], BF16, name="know_rows%d" % image)
+            km = const.tile([P, C], BF16, name="mask_rows%d" % image)
+            nc.scalar.dma_start(out=kk[:], in_=kv_know[image, 0, :].partition_broadcast(P))
+            nc.scalar.dma_start(out=km[:], in_=kv_mask[image, 0, :].partition_broadcast(P))
+            know_rows.append(kk)
+            mask_rows.append(km)
+        bo_rows = const.tile([P, C], BF16, name="bo_rows")
+        nc.scalar.dma_start(out=bo_rows[:], in_=b_out.partition_broadcast(P))
+
+        ident_f32 = const.tile([P, P], F32, name="ident_f32")
+        make_identity(nc, ident_f32[:])
+        ident_bf16 = const.tile([P, P], BF16, name="ident_bf16")
+        make_identity(nc, ident_bf16[:])
+
+        cols_ps = psum_g.tile([P, P], BF16, name="cols_ps", tag="g_cp")
+        nc.tensor.transpose(cols_ps[:], rows_in[:], ident_bf16[:])
+        cols = const.tile([P, P], F32, name="cols")
+        nc.vector.tensor_copy(out=cols[:], in_=cols_ps[:])
+        n_tiles = GROUPS * TILES
+        m = cols[:, 0:n_tiles]
+        bq = cols[:, n_tiles : n_tiles + BLOCKS]
+
+        def per_pixel(label):
+            return const.tile([P, n_tiles], F32, name=label)
+
+        inv = per_pixel("inv")
+        nc.vector.tensor_scalar(out=inv[:], in0=m, scalar1=-1.0, scalar2=1.0, op0=ALU.mult, op1=ALU.add)
+        mixed = per_pixel("mixed")
+        nc.vector.scalar_tensor_tensor(out=mixed[:], in0=m, scalar=0.3, in1=inv[:], op0=ALU.mult, op1=ALU.add)
+        w_know = per_pixel("w_know")
+        nc.vector.tensor_tensor(out=w_know[:], in0=mixed[:], in1=inv[:], op=ALU.mult)
+        w_mask = per_pixel("w_mask")
+        nc.vector.scalar_tensor_tensor(out=w_mask[:], in0=m, scalar=0.7, in1=m, op0=ALU.mult, op1=ALU.mult)
+        w_sum = per_pixel("w_sum")
+        nc.vector.tensor_tensor(out=w_sum[:], in0=w_know[:], in1=w_mask[:], op=ALU.add)
+        r_sum = per_pixel("r_sum")
+        nc.vector.reciprocal(out=r_sum[:], in_=w_sum[:])
+        share = per_pixel("share")
+        nc.vector.tensor_tensor(out=share[:], in0=w_mask[:], in1=r_sum[:], op=ALU.mult)
+        r_sum2 = per_pixel("r_sum2")
+        nc.vector.tensor_tensor(out=r_sum2[:], in0=r_sum[:], in1=r_sum[:], op=ALU.mult)
+
+        diff_rows = []
+        for image in range(IMAGES):
+            diff = const.tile([P, C], F32, name="diff_rows%d" % image)
+            nc.vector.tensor_tensor(out=diff[:], in0=mask_rows[image][:], in1=know_rows[image][:], op=ALU.subtract)
+            diff_rows.append(diff)
+
+        x_quant, q_by_channel, g_quant = {}, {}, {}
+
+        def quantise_x(g):
+            chunk, part = divmod(g, GROUPS_PER_CHUNK)
+            grouped = work.tile([P, GROUP, PACK], BF16, name="x_grouped", align_bytes=64)
+            nc.scalar.copy(
+                out=grouped[:].rearrange("p (c i) t -> p c t i", i=RUN),
+                in_=x_raw[chunk][:, :, part * GROUP : (part + 1) * GROUP].rearrange("p t (c i) -> p c t i", i=RUN),
+            )
+            codes = work.tile([P, GROUP], U32, name="x_codes", align_bytes=64)
+            plane = work.tile([P, GROUP], U8, name="x_plane", align_bytes=64)
+            nc.vector.quantize_mx(
+                out=codes[:].bitcast(FP8X4), scales=plane[:], in_=grouped[:].rearrange("p w t -> p (w t)")
+            )
+            x_quant[g] = (codes, plane)
+
+        def project_q(g):
+            codes, plane = x_quant.pop(g)
+            q_cp = work.tile([P, BLOCKS, GROUP], F32, name="q_cp")
+            for j in range(BLOCKS):
+                block = slice(j * P, (j + 1) * P)
+                acc = psum_q.tile([P, GROUP], F32, name="q_acc")
+                nc.tensor.matmul_mx(
+                    out=acc[:],
+                    lhsT=wq_codes[:, block].bitcast(FP8X4),
+                    lhsT_scale=wq_plane[:, block],
+                    rhs=codes[:].bitcast(FP8X4),
+                    rhs_scale=plane[:],
+                    start=True,
+                    stop=True,
+                )
+                nc.scalar.activation(out=q_cp[:, j, :], in_=acc[:], func=ACT.Identity, bias=bq[:, j : j + 1], scale=1.0)
+            q_by_channel[g] = q_cp
+
+        def gate(g):
+            image = g // GROUPS_PER_IMAGE
+            q_cp = q_by_channel.pop(g)
+            grouped = work.tile([P, TILES, P, PACK], BF16, name="g_grouped", align_bytes=64)
+            grouped_words = grouped[:].bitcast(F32)
+            for i in range(TILES):
+                t = g * TILES + i
+                q_pp = psum_t.tile([P, C], F32, name="q_pp")
+                for j in range(BLOCKS):
+                    nc.tensor.transpose(q_pp[:, j * P : (j + 1) * P], q_cp[:, j, i * P : (i + 1) * P], ident_f32[:])
+                squares = tiles3.tile([P, C], BF16, name="squares")
+                norm2 = small.tile([P, 1], F32, name="norm2")
+                nc.scalar.activation(out=squares[:], in_=q_pp[:], func=ACT.Square, accum_out=norm2[:])
+                ratio = small.tile([P, 1], F32, name="ratio")
+                nc.scalar.activation(out=ratio[:], in_=norm2[:], func=ACT.Sqrt, scale=r_sum2[:, t : t + 1])
+                scale = small.tile([P, 1], F32, name="scale")
+                nc.vector.reciprocal(out=scale[:], in_=ratio[:])
+                blend = tiles3.tile([P, C], F32, name="blend")
+                nc.vector.scalar_tensor_tensor(
+                    out=blend[:], in0=diff_rows[image][:], scalar=share[:, t : t + 1], in1=know_rows[image][:],
+                    op0=ALU.mult, op1=ALU.add,
+                )
+                g_pp = tiles3.tile([P, C], BF16, name="g_pp")
+                nc.vector.scalar_tensor_tensor(
+                    out=g_pp[:], in0=q_pp[:], scalar=scale[:], in1=blend[:], op0=ALU.mult, op1=ALU.mult
+                )
+                if i % 2 == 0:
+                    g_cp = psum_g.tile([P, 2, 2, P], F32, name="g_cp")
+                words = g_pp[:].bitcast(F32)
+                for u in range(2):
+                    nc.tensor.transpose(g_cp[:, i % 2, u, :], words[:, u : C // 2 : 2], ident_f32[:])
+                if i % 2 == 1:
+                    nc.scalar.copy(out=grouped_words[:, i - 1 : i + 1, :, :], in_=g_cp[:].rearrange("p i u w -> p i w u"))
+            codes = work.tile([P, GROUP], U32, name="g_codes", align_bytes=64)
+            plane = work.tile([P, GROUP], U8, name="g_plane", align_bytes=64)
+            nc.vector.quantize_mx(
+                out=codes[:].bitcast(FP8X4), scales=plane[:], in_=grouped[:].rearrange("p i w t -> p (i w t)")
+            )
+            g_quant[g] = (codes, plane)
+
+        def project_out(g):
+            image, part = divmod(g, GROUPS_PER_IMAGE)
+            codes, plane = g_quant.pop(g)
+            y_sb = tiles3.tile([P, TILES, C], F32, name="y_sb")
+            for i in range(TILES):
+                pixels = slice(i * P, (i + 1) * P)
+                acc = psum_y.tile([P, C], F32, name="y_acc")
+                nc.tensor.matmul_mx(
+                    out=acc[:],
+                    lhsT=codes[:, pixels].bitcast(FP8X4),
+                    lhsT_scale=plane[:, pixels],
+                    rhs=wo_codes[:].bitcast(FP8X4),
+                    rhs_scale=wo_plane[:],
+                    start=True,
+                    stop=True,
+                )
+                nc.vector.tensor_tensor(out=y_sb[:, i, :], in0=acc[:], in1=bo_rows[:], op=ALU.add)
+            nc.sync.dma_start(
+                out=out[image, part * GROUP : (part + 1) * GROUP, :].rearrange("(i p) c -> p i c", p=P), in_=y_sb[:]
+            )
+
+        stages = [quantise_x, project_q, gate, project_out]
+        for step in range(GROUPS + len(stages) - 1):
+            for depth in reversed(range(len(stages))):
+                if 0 <= step - depth < GROUPS:
+                    stages[depth](step - depth)

@@ -17,14 +17,15 @@ PACK = 4
 IMAGES = 2
 C = 512
 PIXELS = 4096
-GROUP = 512
-TILES = GROUP // P
 BLOCKS = C // P
+GROUP = 512
+TILES_PER_GROUP = GROUP // P
 GROUPS_PER_IMAGE = PIXELS // GROUP
 GROUPS = IMAGES * GROUPS_PER_IMAGE
-CHUNK = 1024
-GROUPS_PER_CHUNK = CHUNK // GROUP
+ALL_TILES = GROUPS * TILES_PER_GROUP
+TILES_PER_IMAGE = ALL_TILES // IMAGES
 RUN = 4
+BLEND_LEAD = 6
 
 FLOPS = 2 * 2 * IMAGES * PIXELS * C * C
 
@@ -48,9 +49,10 @@ def tile_hydraattention_pb_t_kernel(
     nc = tc.nc
     with ExitStack() as stack:
         const = stack.enter_context(tc.tile_pool(name="const", bufs=1))
-        x_pool = stack.enter_context(tc.tile_pool(name="x_pool", bufs=IMAGES * PIXELS // CHUNK))
-        work = stack.enter_context(tc.tile_pool(name="work", bufs=2))
-        tiles3 = stack.enter_context(tc.tile_pool(name="tiles3", bufs=3))
+        x_pool = stack.enter_context(tc.tile_pool(name="x_pool", bufs=GROUPS))
+        stream2 = stack.enter_context(tc.tile_pool(name="stream2", bufs=2))
+        stream3 = stack.enter_context(tc.tile_pool(name="stream3", bufs=3))
+        blends = stack.enter_context(tc.tile_pool(name="blends", bufs=BLEND_LEAD + 2))
         small = stack.enter_context(tc.tile_pool(name="small", bufs=4))
         psum_q = stack.enter_context(tc.psum_pool(name="psum_q", bufs=2))
         psum_t = stack.enter_context(tc.psum_pool(name="psum_t", bufs=3))
@@ -58,18 +60,19 @@ def tile_hydraattention_pb_t_kernel(
         psum_y = stack.enter_context(tc.psum_pool(name="psum_y", bufs=2))
 
         x_raw = []
-        for chunk in range(IMAGES * PIXELS // CHUNK):
-            image, part = divmod(chunk, PIXELS // CHUNK)
-            raw = x_pool.tile([P, PACK, CHUNK], BF16, name="x_raw")
+        for g in range(GROUPS):
+            image, part = divmod(g, GROUPS_PER_IMAGE)
+            raw = x_pool.tile([P, PACK, GROUP], BF16, name="x_raw")
             x_raw.append(raw)
             rows = x[image].rearrange("(p t) h w -> p t (h w)", t=PACK)
-            nc.sync.dma_start(out=raw[:], in_=rows[:, :, part * CHUNK : (part + 1) * CHUNK])
-            if chunk == 0:
-                wq_codes, wq_plane = load_weight(nc, const, W_q_words, W_q_scales, "wq")
+            nc.sync.dma_start(out=raw[:], in_=rows[:, :, part * GROUP : (part + 1) * GROUP])
+            if g == 0:
                 rows_in = const.tile([P, P], BF16, name="rows_in")
                 nc.vector.memset(rows_in[:], 0.0)
                 nc.sync.dma_start(out=rows_in[0:64, :], in_=mask.rearrange("b o (r a) w -> (b o r) (a w)", a=2))
                 nc.sync.dma_start(out=rows_in[64:68, :], in_=b_q.rearrange("(j m) -> j m", m=P))
+                wq_codes, wq_plane = load_weight(nc, const, W_q_words, W_q_scales, "wq")
+            if g == 1:
                 wo_codes, wo_plane = load_weight(nc, const, W_out_words, W_out_scales, "wo")
 
         know_rows, mask_rows = [], []
@@ -83,21 +86,20 @@ def tile_hydraattention_pb_t_kernel(
         bo_rows = const.tile([P, C], BF16, name="bo_rows")
         nc.scalar.dma_start(out=bo_rows[:], in_=b_out.partition_broadcast(P))
 
-        ident_f32 = const.tile([P, P], F32, name="ident_f32")
-        make_identity(nc, ident_f32[:])
         ident_bf16 = const.tile([P, P], BF16, name="ident_bf16")
         make_identity(nc, ident_bf16[:])
+        ident_f32 = const.tile([P, P], F32, name="ident_f32")
+        make_identity(nc, ident_f32[:])
 
         cols_ps = psum_g.tile([P, P], BF16, name="cols_ps", tag="g_cp")
         nc.tensor.transpose(cols_ps[:], rows_in[:], ident_bf16[:])
         cols = const.tile([P, P], F32, name="cols")
         nc.vector.tensor_copy(out=cols[:], in_=cols_ps[:])
-        n_tiles = GROUPS * TILES
-        m = cols[:, 0:n_tiles]
-        bq = cols[:, n_tiles : n_tiles + BLOCKS]
+        m = cols[:, 0:ALL_TILES]
+        bq = cols[:, ALL_TILES : ALL_TILES + BLOCKS]
 
         def per_pixel(label):
-            return const.tile([P, n_tiles], F32, name=label)
+            return const.tile([P, ALL_TILES], F32, name=label)
 
         inv = per_pixel("inv")
         nc.vector.tensor_scalar(out=inv[:], in0=m, scalar1=-1.0, scalar2=1.0, op0=ALU.mult, op1=ALU.add)
@@ -122,103 +124,175 @@ def tile_hydraattention_pb_t_kernel(
             nc.vector.tensor_tensor(out=diff[:], in0=mask_rows[image][:], in1=know_rows[image][:], op=ALU.subtract)
             diff_rows.append(diff)
 
-        x_quant, q_by_channel, g_quant = {}, {}, {}
+        x_grouped, x_quant, q_acc, q_cp, q_pp, norm2, scale = {}, {}, {}, {}, {}, {}, {}
+        blend, g_pp, g_cp, g_grouped, g_quant, y_acc, y_sb = {}, {}, {}, {}, {}, {}, {}
 
-        def quantise_x(g):
-            chunk, part = divmod(g, GROUPS_PER_CHUNK)
-            grouped = work.tile([P, GROUP, PACK], BF16, name="x_grouped", align_bytes=64)
+        def is_tile(t):
+            return 0 <= t < ALL_TILES
+
+        def regroup_x(t):
+            if not is_tile(t):
+                return
+            g, i = divmod(t, TILES_PER_GROUP)
+            if i == 0:
+                x_grouped[g] = stream2.tile([P, GROUP, PACK], BF16, name="x_grouped", align_bytes=64)
+            pixels = slice(i * P, (i + 1) * P)
             nc.scalar.copy(
-                out=grouped[:].rearrange("p (c i) t -> p c t i", i=RUN),
-                in_=x_raw[chunk][:, :, part * GROUP : (part + 1) * GROUP].rearrange("p t (c i) -> p c t i", i=RUN),
+                out=x_grouped[g][:, pixels, :].rearrange("p (c i) t -> p c t i", i=RUN),
+                in_=x_raw[g][:, :, pixels].rearrange("p t (c i) -> p c t i", i=RUN),
             )
-            codes = work.tile([P, GROUP], U32, name="x_codes", align_bytes=64)
-            plane = work.tile([P, GROUP], U8, name="x_plane", align_bytes=64)
+
+        def quantise_x(t):
+            if not is_tile(t) or t % TILES_PER_GROUP != 0:
+                return
+            g = t // TILES_PER_GROUP
+            codes = stream2.tile([P, GROUP], U32, name="x_codes", align_bytes=64)
+            plane = stream2.tile([P, GROUP], U8, name="x_plane", align_bytes=64)
             nc.vector.quantize_mx(
-                out=codes[:].bitcast(FP8X4), scales=plane[:], in_=grouped[:].rearrange("p w t -> p (w t)")
+                out=codes[:].bitcast(FP8X4), scales=plane[:], in_=x_grouped.pop(g)[:].rearrange("p w t -> p (w t)")
             )
             x_quant[g] = (codes, plane)
 
-        def project_q(g):
-            codes, plane = x_quant.pop(g)
-            q_cp = work.tile([P, BLOCKS, GROUP], F32, name="q_cp")
+        def project_q(b):
+            if not is_tile(b):
+                return
+            g, j = divmod(b, BLOCKS)
+            codes, plane = x_quant[g]
+            block = slice(j * P, (j + 1) * P)
+            q_acc[b] = psum_q.tile([P, GROUP], F32, name="q_acc")
+            nc.tensor.matmul_mx(
+                out=q_acc[b][:],
+                lhsT=wq_codes[:, block].bitcast(FP8X4),
+                lhsT_scale=wq_plane[:, block],
+                rhs=codes[:].bitcast(FP8X4),
+                rhs_scale=plane[:],
+                start=True,
+                stop=True,
+            )
+
+        def add_bq(b):
+            if not is_tile(b):
+                return
+            g, j = divmod(b, BLOCKS)
+            if j == 0:
+                q_cp[g] = stream3.tile([P, BLOCKS, GROUP], F32, name="q_cp")
+            nc.scalar.activation(
+                out=q_cp[g][:, j, :], in_=q_acc.pop(b)[:], func=ACT.Identity, bias=bq[:, j : j + 1], scale=1.0
+            )
+
+        def transpose_q(t):
+            if not is_tile(t):
+                return
+            g, i = divmod(t, TILES_PER_GROUP)
+            q_pp[t] = psum_t.tile([P, C], F32, name="q_pp")
             for j in range(BLOCKS):
-                block = slice(j * P, (j + 1) * P)
-                acc = psum_q.tile([P, GROUP], F32, name="q_acc")
-                nc.tensor.matmul_mx(
-                    out=acc[:],
-                    lhsT=wq_codes[:, block].bitcast(FP8X4),
-                    lhsT_scale=wq_plane[:, block],
-                    rhs=codes[:].bitcast(FP8X4),
-                    rhs_scale=plane[:],
-                    start=True,
-                    stop=True,
-                )
-                nc.scalar.activation(out=q_cp[:, j, :], in_=acc[:], func=ACT.Identity, bias=bq[:, j : j + 1], scale=1.0)
-            q_by_channel[g] = q_cp
+                nc.tensor.transpose(q_pp[t][:, j * P : (j + 1) * P], q_cp[g][:, j, i * P : (i + 1) * P], ident_f32[:])
 
-        def gate(g):
-            image = g // GROUPS_PER_IMAGE
-            q_cp = q_by_channel.pop(g)
-            grouped = work.tile([P, TILES, P, PACK], BF16, name="g_grouped", align_bytes=64)
-            grouped_words = grouped[:].bitcast(F32)
-            for i in range(TILES):
-                t = g * TILES + i
-                q_pp = psum_t.tile([P, C], F32, name="q_pp")
-                for j in range(BLOCKS):
-                    nc.tensor.transpose(q_pp[:, j * P : (j + 1) * P], q_cp[:, j, i * P : (i + 1) * P], ident_f32[:])
-                squares = tiles3.tile([P, C], BF16, name="squares")
-                norm2 = small.tile([P, 1], F32, name="norm2")
-                nc.scalar.activation(out=squares[:], in_=q_pp[:], func=ACT.Square, accum_out=norm2[:])
-                ratio = small.tile([P, 1], F32, name="ratio")
-                nc.scalar.activation(out=ratio[:], in_=norm2[:], func=ACT.Sqrt, scale=r_sum2[:, t : t + 1])
-                scale = small.tile([P, 1], F32, name="scale")
-                nc.vector.reciprocal(out=scale[:], in_=ratio[:])
-                blend = tiles3.tile([P, C], F32, name="blend")
-                nc.vector.scalar_tensor_tensor(
-                    out=blend[:], in0=diff_rows[image][:], scalar=share[:, t : t + 1], in1=know_rows[image][:],
-                    op0=ALU.mult, op1=ALU.add,
-                )
-                g_pp = tiles3.tile([P, C], BF16, name="g_pp")
-                nc.vector.scalar_tensor_tensor(
-                    out=g_pp[:], in0=q_pp[:], scalar=scale[:], in1=blend[:], op0=ALU.mult, op1=ALU.mult
-                )
-                if i % 2 == 0:
-                    g_cp = psum_g.tile([P, 2, 2, P], F32, name="g_cp")
-                words = g_pp[:].bitcast(F32)
-                for u in range(2):
-                    nc.tensor.transpose(g_cp[:, i % 2, u, :], words[:, u : C // 2 : 2], ident_f32[:])
-                if i % 2 == 1:
-                    nc.scalar.copy(out=grouped_words[:, i - 1 : i + 1, :, :], in_=g_cp[:].rearrange("p i u w -> p i w u"))
-            codes = work.tile([P, GROUP], U32, name="g_codes", align_bytes=64)
-            plane = work.tile([P, GROUP], U8, name="g_plane", align_bytes=64)
+        def sum_squares(t):
+            if not is_tile(t):
+                return
+            squares = stream3.tile([P, C], BF16, name="squares")
+            norm2[t] = small.tile([P, 1], F32, name="norm2")
+            nc.scalar.activation(out=squares[:], in_=q_pp[t][:], func=ACT.Square, accum_out=norm2[t][:])
+
+        def root(t):
+            if not is_tile(t):
+                return
+            ratio = small.tile([P, 1], F32, name="ratio")
+            nc.scalar.activation(out=ratio[:], in_=norm2.pop(t)[:], func=ACT.Sqrt, scale=r_sum2[:, t : t + 1])
+            scale[t] = ratio
+
+        def blend_vectors(t):
+            if not is_tile(t):
+                return
+            image = t // TILES_PER_IMAGE
+            blend[t] = blends.tile([P, C], F32, name="blend")
+            nc.vector.scalar_tensor_tensor(
+                out=blend[t][:], in0=diff_rows[image][:], scalar=share[:, t : t + 1], in1=know_rows[image][:],
+                op0=ALU.mult, op1=ALU.add,
+            )
+
+        def gate(t):
+            if not is_tile(t):
+                return
+            factor = small.tile([P, 1], F32, name="factor")
+            nc.vector.reciprocal(out=factor[:], in_=scale.pop(t)[:])
+            g_pp[t] = stream3.tile([P, C], BF16, name="g_pp")
+            nc.vector.scalar_tensor_tensor(
+                out=g_pp[t][:], in0=q_pp.pop(t)[:], scalar=factor[:], in1=blend.pop(t)[:], op0=ALU.mult, op1=ALU.mult
+            )
+
+        def transpose_g(t):
+            if not is_tile(t):
+                return
+            pair, half = divmod(t, 2)
+            if half == 0:
+                g_cp[pair] = psum_g.tile([P, 2, 2, P], F32, name="g_cp")
+            words = g_pp.pop(t)[:].bitcast(F32)
+            for u in range(2):
+                nc.tensor.transpose(g_cp[pair][:, half, u, :], words[:, u : C // 2 : 2], ident_f32[:])
+
+        def regroup_g(t):
+            if not is_tile(t) or t % 2 == 0:
+                return
+            pair = t // 2
+            g_grouped[pair] = stream3.tile([P, 2, P, PACK], BF16, name="g_grouped", align_bytes=64)
+            nc.scalar.copy(out=g_grouped[pair][:].bitcast(F32), in_=g_cp.pop(pair)[:].rearrange("p i u w -> p i w u"))
+
+        def quantise_g(t):
+            if not is_tile(t) or t % 2 == 0:
+                return
+            pair = t // 2
+            codes = stream3.tile([P, 2 * P], U32, name="g_codes", align_bytes=64)
+            plane = stream3.tile([P, 2 * P], U8, name="g_plane", align_bytes=64)
             nc.vector.quantize_mx(
-                out=codes[:].bitcast(FP8X4), scales=plane[:], in_=grouped[:].rearrange("p i w t -> p (i w t)")
+                out=codes[:].bitcast(FP8X4), scales=plane[:],
+                in_=g_grouped.pop(pair)[:].rearrange("p i w t -> p (i w t)"),
             )
-            g_quant[g] = (codes, plane)
+            g_quant[pair] = (codes, plane)
 
-        def project_out(g):
-            image, part = divmod(g, GROUPS_PER_IMAGE)
-            codes, plane = g_quant.pop(g)
-            y_sb = tiles3.tile([P, TILES, C], F32, name="y_sb")
-            for i in range(TILES):
-                pixels = slice(i * P, (i + 1) * P)
-                acc = psum_y.tile([P, C], F32, name="y_acc")
-                nc.tensor.matmul_mx(
-                    out=acc[:],
-                    lhsT=codes[:, pixels].bitcast(FP8X4),
-                    lhsT_scale=plane[:, pixels],
-                    rhs=wo_codes[:].bitcast(FP8X4),
-                    rhs_scale=wo_plane[:],
-                    start=True,
-                    stop=True,
-                )
-                nc.vector.tensor_tensor(out=y_sb[:, i, :], in0=acc[:], in1=bo_rows[:], op=ALU.add)
-            nc.sync.dma_start(
-                out=out[image, part * GROUP : (part + 1) * GROUP, :].rearrange("(i p) c -> p i c", p=P), in_=y_sb[:]
+        def project_out(t):
+            if not is_tile(t):
+                return
+            pair, half = divmod(t, 2)
+            codes, plane = g_quant[pair]
+            pixels = slice(half * P, (half + 1) * P)
+            y_acc[t] = psum_y.tile([P, C], F32, name="y_acc")
+            nc.tensor.matmul_mx(
+                out=y_acc[t][:],
+                lhsT=codes[:, pixels].bitcast(FP8X4),
+                lhsT_scale=plane[:, pixels],
+                rhs=wo_codes[:].bitcast(FP8X4),
+                rhs_scale=wo_plane[:],
+                start=True,
+                stop=True,
             )
 
-        stages = [quantise_x, project_q, gate, project_out]
-        for step in range(GROUPS + len(stages) - 1):
-            for depth in reversed(range(len(stages))):
-                if 0 <= step - depth < GROUPS:
-                    stages[depth](step - depth)
+        def add_bo_and_store(t):
+            if not is_tile(t):
+                return
+            pair, half = divmod(t, 2)
+            if half == 0:
+                y_sb[pair] = stream3.tile([P, 2, C], F32, name="y_sb")
+            nc.vector.tensor_tensor(out=y_sb[pair][:, half, :], in0=y_acc.pop(t)[:], in1=bo_rows[:], op=ALU.add)
+            if half == 1:
+                rows = out.flatten_outer_dims()[pair * 2 * P : (pair + 1) * 2 * P, :]
+                nc.sync.dma_start(out=rows.rearrange("(i p) c -> p i c", p=P), in_=y_sb.pop(pair)[:])
+
+        for s in range(-10, ALL_TILES + 6 + 1):
+            transpose_q(s)
+            transpose_g(s - 2)
+            project_q(s + 5)
+            project_out(s - 5)
+
+            add_bq(s + 4)
+            sum_squares(s)
+            regroup_g(s - 2)
+            regroup_x(s + 10)
+            root(s)
+
+            gate(s - 1)
+            add_bo_and_store(s - 6)
+            blend_vectors(s + BLEND_LEAD)
+            quantise_g(s - 3)
+            quantise_x(s + 6)

@@ -25,6 +25,7 @@ GROUPS = IMAGES * GROUPS_PER_IMAGE
 ALL_TILES = GROUPS * TILES_PER_GROUP
 TILES_PER_IMAGE = ALL_TILES // IMAGES
 RUN = 4
+VECTOR_GROUPS = 3
 BLEND_LEAD = 6
 
 FLOPS = 2 * 2 * IMAGES * PIXELS * C * C
@@ -137,7 +138,8 @@ def tile_hydraattention_pb_t_kernel(
             if i == 0:
                 x_grouped[g] = stream2.tile([P, GROUP, PACK], BF16, name="x_grouped", align_bytes=64)
             pixels = slice(i * P, (i + 1) * P)
-            nc.scalar.copy(
+            copy = nc.vector.tensor_copy if g < VECTOR_GROUPS else nc.scalar.copy
+            copy(
                 out=x_grouped[g][:, pixels, :].rearrange("p (c i) t -> p c t i", i=RUN),
                 in_=x_raw[g][:, :, pixels].rearrange("p t (c i) -> p c t i", i=RUN),
             )
@@ -198,9 +200,10 @@ def tile_hydraattention_pb_t_kernel(
         def root(t):
             if not is_tile(t):
                 return
-            ratio = small.tile([P, 1], F32, name="ratio")
-            nc.scalar.activation(out=ratio[:], in_=norm2.pop(t)[:], func=ACT.Sqrt, scale=r_sum2[:, t : t + 1])
-            scale[t] = ratio
+            scale[t] = small.tile([P, 1], F32, name="scale")
+            nc.scalar.activation(
+                out=scale[t][:], in_=norm2.pop(t)[:], func=ACT.Abs_reciprocal_sqrt, scale=r_sum2[:, t : t + 1]
+            )
 
         def blend_vectors(t):
             if not is_tile(t):
@@ -215,11 +218,9 @@ def tile_hydraattention_pb_t_kernel(
         def gate(t):
             if not is_tile(t):
                 return
-            factor = small.tile([P, 1], F32, name="factor")
-            nc.vector.reciprocal(out=factor[:], in_=scale.pop(t)[:])
             g_pp[t] = stream3.tile([P, C], BF16, name="g_pp")
             nc.vector.scalar_tensor_tensor(
-                out=g_pp[t][:], in0=q_pp.pop(t)[:], scalar=factor[:], in1=blend.pop(t)[:], op0=ALU.mult, op1=ALU.mult
+                out=g_pp[t][:], in0=q_pp.pop(t)[:], scalar=scale.pop(t)[:], in1=blend.pop(t)[:], op0=ALU.mult, op1=ALU.mult
             )
 
         def transpose_g(t):

@@ -60,6 +60,14 @@ def tile_hydraattention_pb_t_kernel(
         psum_g = stack.enter_context(tc.psum_pool(name="psum_g", bufs=1))
         psum_y = stack.enter_context(tc.psum_pool(name="psum_y", bufs=2))
 
+        warm = const.tile([P, 2], F32, name="warm")
+        nc.gpsimd.memset(warm[:], 1.0)
+        nc.scalar.activation(out=warm[:, 1:2], in_=warm[:, 0:1], func=ACT.Abs_reciprocal_sqrt)
+
+        rows_in = const.tile([P, P], BF16, name="rows_in")
+        nc.vector.memset(rows_in[:], 0.0)
+        nc.sync.dma_start(out=rows_in[0:64, :], in_=mask.rearrange("b o (r a) w -> (b o r) (a w)", a=2))
+        nc.sync.dma_start(out=rows_in[64:68, :], in_=b_q.rearrange("(j m) -> j m", m=P))
         x_raw = []
         for g in range(GROUPS):
             image, part = divmod(g, GROUPS_PER_IMAGE)
@@ -68,10 +76,6 @@ def tile_hydraattention_pb_t_kernel(
             rows = x[image].rearrange("(p t) h w -> p t (h w)", t=PACK)
             nc.sync.dma_start(out=raw[:], in_=rows[:, :, part * GROUP : (part + 1) * GROUP])
             if g == 0:
-                rows_in = const.tile([P, P], BF16, name="rows_in")
-                nc.vector.memset(rows_in[:], 0.0)
-                nc.sync.dma_start(out=rows_in[0:64, :], in_=mask.rearrange("b o (r a) w -> (b o r) (a w)", a=2))
-                nc.sync.dma_start(out=rows_in[64:68, :], in_=b_q.rearrange("(j m) -> j m", m=P))
                 wq_codes, wq_plane = load_weight(nc, const, W_q_words, W_q_scales, "wq")
             if g == 1:
                 wo_codes, wo_plane = load_weight(nc, const, W_out_words, W_out_scales, "wo")
@@ -80,8 +84,9 @@ def tile_hydraattention_pb_t_kernel(
         for image in range(IMAGES):
             kk = const.tile([P, C], BF16, name="know_rows%d" % image)
             km = const.tile([P, C], BF16, name="mask_rows%d" % image)
-            nc.scalar.dma_start(out=kk[:], in_=kv_know[image, 0, :].partition_broadcast(P))
-            nc.scalar.dma_start(out=km[:], in_=kv_mask[image, 0, :].partition_broadcast(P))
+            queue = nc.scalar if image == 0 else nc.sync
+            queue.dma_start(out=kk[:], in_=kv_know[image, 0, :].partition_broadcast(P))
+            queue.dma_start(out=km[:], in_=kv_mask[image, 0, :].partition_broadcast(P))
             know_rows.append(kk)
             mask_rows.append(km)
         bo_rows = const.tile([P, C], BF16, name="bo_rows")
@@ -276,7 +281,9 @@ def tile_hydraattention_pb_t_kernel(
             if half == 0:
                 y_sb[pair] = stream3.tile([P, 2, C], F32, name="y_sb")
             nc.vector.tensor_tensor(out=y_sb[pair][:, half, :], in0=y_acc.pop(t)[:], in1=bo_rows[:], op=ALU.add)
-            if half == 1:
+            if pair == ALL_TILES // 2 - 1:
+                nc.sync.dma_start(out=out.flatten_outer_dims()[t * P : (t + 1) * P, :], in_=y_sb[pair][:, half, :])
+            elif half == 1:
                 rows = out.flatten_outer_dims()[pair * 2 * P : (pair + 1) * 2 * P, :]
                 nc.sync.dma_start(out=rows.rearrange("(i p) c -> p i c", p=P), in_=y_sb.pop(pair)[:])
 

@@ -27,6 +27,10 @@ TILES_PER_IMAGE = ALL_TILES // IMAGES
 RUN = 4
 VECTOR_GROUPS = 3
 BLEND_LEAD = 6
+PIECES = 3
+EVERY = 2
+BY_TENSOR = ALL_TILES // EVERY
+ROW_BLOCK = 8
 
 FLOPS = 2 * 2 * IMAGES * PIXELS * C * C
 
@@ -92,6 +96,18 @@ def tile_hydraattention_pb_t_kernel(
         bo_rows = const.tile([P, C], BF16, name="bo_rows")
         nc.scalar.dma_start(out=bo_rows[:], in_=b_out.partition_broadcast(P))
 
+        vector_rows = []
+        for image in range(IMAGES):
+            vr = const.tile([P, C], BF16, name="vector_rows%d" % image)
+            nc.vector.memset(vr[:], 0.0)
+            queue = nc.scalar if image == 0 else nc.sync
+            queue.dma_start(out=vr[0:1, :], in_=kv_know[image, 0:1, :])
+            queue.dma_start(out=vr[1 : 1 + PIECES, :], in_=kv_mask[image, 0, :].partition_broadcast(PIECES))
+            queue.dma_start(out=vr[1 + PIECES : 1 + 2 * PIECES, :], in_=kv_know[image, 0, :].partition_broadcast(PIECES))
+            vector_rows.append(vr)
+        factors = const.tile([P, BY_TENSOR, P], BF16, name="factors")
+        nc.vector.memset(factors[:].rearrange("p n r -> p (n r)").bitcast(I32), 0)
+
         ident_bf16 = const.tile([P, P], BF16, name="ident_bf16")
         make_identity(nc, ident_bf16[:])
         ident_f32 = const.tile([P, P], F32, name="ident_f32")
@@ -124,6 +140,19 @@ def tile_hydraattention_pb_t_kernel(
         r_sum2 = per_pixel("r_sum2")
         nc.vector.tensor_tensor(out=r_sum2[:], in0=r_sum[:], in1=r_sum[:], op=ALU.mult)
 
+        nc.vector.memset(factors[:, :, 0], 1.0)
+        rest = share[:, EVERY - 1 : ALL_TILES : EVERY]
+        for r in range(PIECES):
+            nc.vector.tensor_copy(out=factors[:, :, 1 + r], in_=rest)
+            nc.vector.tensor_scalar(
+                out=factors[:, :, 1 + PIECES + r], in0=factors[:, :, 1 + r], scalar1=-1.0, scalar2=0.0, op0=ALU.mult, op1=ALU.add
+            )
+            if r < PIECES - 1:
+                left = const.tile([P, BY_TENSOR], F32, name="left%d" % r)
+                nc.vector.tensor_tensor(out=left[:], in0=rest, in1=factors[:, :, 1 + r], op=ALU.subtract)
+                rest = left[:]
+        factor_rows = const.tile([P, BY_TENSOR, P], BF16, name="factor_rows")
+
         diff_rows = []
         for image in range(IMAGES):
             diff = const.tile([P, C], F32, name="diff_rows%d" % image)
@@ -132,6 +161,13 @@ def tile_hydraattention_pb_t_kernel(
 
         x_grouped, x_quant, q_acc, q_cp, q_pp, norm2, scale = {}, {}, {}, {}, {}, {}, {}
         blend, g_pp, g_cp, g_grouped, g_quant, y_acc, y_sb = {}, {}, {}, {}, {}, {}, {}
+        rows_ps, blend_ps = {}, {}
+
+        def by_tensor(t):
+            return is_tile(t) and t % EVERY == EVERY - 1
+
+        def starts_rows(t):
+            return is_tile(t) and t % (EVERY * ROW_BLOCK) == 0
 
         def is_tile(t):
             return 0 <= t < ALL_TILES
@@ -143,11 +179,17 @@ def tile_hydraattention_pb_t_kernel(
             if i == 0:
                 x_grouped[g] = stream2.tile([P, GROUP, PACK], BF16, name="x_grouped", align_bytes=64)
             pixels = slice(i * P, (i + 1) * P)
-            copy = nc.vector.tensor_copy if g < VECTOR_GROUPS else nc.scalar.copy
-            copy(
-                out=x_grouped[g][:, pixels, :].rearrange("p (c i) t -> p c t i", i=RUN),
-                in_=x_raw[g][:, :, pixels].rearrange("p t (c i) -> p c t i", i=RUN),
-            )
+            if g < VECTOR_GROUPS:
+                nc.vector.tensor_copy(
+                    out=x_grouped[g][:, pixels, :].rearrange("p (c i) t -> p c t i", i=RUN),
+                    in_=x_raw[g][:, :, pixels].rearrange("p t (c i) -> p c t i", i=RUN),
+                )
+            else:
+                nc.gpsimd.tensor_scalar(
+                    out=x_grouped[g][:, pixels, :],
+                    in0=x_raw[g][:, :, pixels].rearrange("p t w -> p w t"),
+                    scalar1=1.0, scalar2=0.0, op0=ALU.mult, op1=ALU.add,
+                )
 
         def quantise_x(t):
             if not is_tile(t) or t % TILES_PER_GROUP != 0:
@@ -211,7 +253,7 @@ def tile_hydraattention_pb_t_kernel(
             )
 
         def blend_vectors(t):
-            if not is_tile(t):
+            if not is_tile(t) or by_tensor(t):
                 return
             image = t // TILES_PER_IMAGE
             blend[t] = blends.tile([P, C], F32, name="blend")
@@ -219,6 +261,34 @@ def tile_hydraattention_pb_t_kernel(
                 out=blend[t][:], in0=diff_rows[image][:], scalar=share[:, t : t + 1], in1=know_rows[image][:],
                 op0=ALU.mult, op1=ALU.add,
             )
+
+        def transpose_factors(t):
+            if not starts_rows(t):
+                return
+            first = t // EVERY
+            rows_ps[t] = psum_y.tile([P, ROW_BLOCK, P], BF16, name="rows_ps", tag="y_acc")
+            for i in range(ROW_BLOCK):
+                nc.tensor.transpose(rows_ps[t][:, i, :], factors[:, first + i, :], ident_bf16[:])
+
+        def copy_factors(t):
+            if not starts_rows(t):
+                return
+            first = t // EVERY
+            nc.scalar.copy(out=factor_rows[:, first : first + ROW_BLOCK, :], in_=rows_ps.pop(t)[:])
+
+        def blend_matmul(t):
+            if not by_tensor(t):
+                return
+            blend_ps[t] = psum_y.tile([P, C], F32, name="blend_ps", tag="y_acc")
+            nc.tensor.matmul(
+                out=blend_ps[t][:], lhsT=factor_rows[:, t // EVERY, :], rhs=vector_rows[t // TILES_PER_IMAGE][:], start=True, stop=True
+            )
+
+        def copy_blend(t):
+            if not by_tensor(t):
+                return
+            blend[t] = blends.tile([P, C], F32, name="blend")
+            nc.scalar.copy(out=blend[t][:], in_=blend_ps.pop(t)[:])
 
         def gate(t):
             if not is_tile(t):
@@ -292,8 +362,12 @@ def tile_hydraattention_pb_t_kernel(
             transpose_g(s - 2)
             project_q(s + 5)
             project_out(s - 5)
+            blend_matmul(s + BLEND_LEAD + 1)
+            transpose_factors(s + BLEND_LEAD + 4)
 
             add_bq(s + 4)
+            copy_blend(s + BLEND_LEAD)
+            copy_factors(s + BLEND_LEAD + 3)
             sum_squares(s)
             regroup_g(s - 2)
             regroup_x(s + 10)

@@ -26,7 +26,7 @@ ALL_TILES = GROUPS * TILES_PER_GROUP
 TILES_PER_IMAGE = ALL_TILES // IMAGES
 RUN = 4
 VECTOR_GROUPS = 3
-BLEND_LEAD = 6
+BLEND_LEAD = 7
 PIECES = 3
 EVERY = 2
 BY_TENSOR = ALL_TILES // EVERY
@@ -192,15 +192,19 @@ def tile_hydraattention_pb_t_kernel(
                 )
 
         def quantise_x(t):
-            if not is_tile(t) or t % TILES_PER_GROUP != 0:
+            if not is_tile(t) or t % 2 != 0:
                 return
-            g = t // TILES_PER_GROUP
-            codes = stream2.tile([P, GROUP], U32, name="x_codes", align_bytes=64)
-            plane = stream2.tile([P, GROUP], U8, name="x_plane", align_bytes=64)
+            g, i = divmod(t, TILES_PER_GROUP)
+            if i == 0:
+                codes = stream2.tile([P, GROUP], U32, name="x_codes", align_bytes=64)
+                plane = stream2.tile([P, GROUP], U8, name="x_plane", align_bytes=64)
+                x_quant[g] = (codes, plane)
+            codes, plane = x_quant[g]
+            pixels = slice(i * P, (i + 2) * P)
             nc.vector.quantize_mx(
-                out=codes[:].bitcast(FP8X4), scales=plane[:], in_=x_grouped.pop(g)[:].rearrange("p w t -> p (w t)")
+                out=codes[:, pixels].bitcast(FP8X4), scales=plane[:, pixels],
+                in_=x_grouped[g][:, pixels, :].rearrange("p w t -> p (w t)"),
             )
-            x_quant[g] = (codes, plane)
 
         def project_q(b):
             if not is_tile(b):
@@ -274,7 +278,7 @@ def tile_hydraattention_pb_t_kernel(
             if not starts_rows(t):
                 return
             first = t // EVERY
-            nc.scalar.copy(out=factor_rows[:, first : first + ROW_BLOCK, :], in_=rows_ps.pop(t)[:])
+            nc.vector.tensor_copy(out=factor_rows[:, first : first + ROW_BLOCK, :], in_=rows_ps.pop(t)[:])
 
         def blend_matmul(t):
             if not by_tensor(t):
@@ -357,7 +361,7 @@ def tile_hydraattention_pb_t_kernel(
                 rows = out.flatten_outer_dims()[pair * 2 * P : (pair + 1) * 2 * P, :]
                 nc.sync.dma_start(out=rows.rearrange("(i p) c -> p i c", p=P), in_=y_sb.pop(pair)[:])
 
-        for s in range(-10, ALL_TILES + 6 + 1):
+        for s in range(-BLEND_LEAD - 4, ALL_TILES + 6 + 1):
             transpose_q(s)
             transpose_g(s - 2)
             project_q(s + 5)
@@ -377,4 +381,4 @@ def tile_hydraattention_pb_t_kernel(
             add_bo_and_store(s - 6)
             blend_vectors(s + BLEND_LEAD)
             quantise_g(s - 3)
-            quantise_x(s + 6)
+            quantise_x(s + 8)

@@ -24,13 +24,12 @@ GROUPS_PER_IMAGE = PIXELS // GROUP
 GROUPS = IMAGES * GROUPS_PER_IMAGE
 ALL_TILES = GROUPS * TILES_PER_GROUP
 TILES_PER_IMAGE = ALL_TILES // IMAGES
+AHEAD = 5
 RUN = 4
-VECTOR_GROUPS = 3
-BLEND_LEAD = 7
+VECTOR_GROUPS = 8
 PIECES = 3
-EVERY = 2
-BY_TENSOR = ALL_TILES // EVERY
-ROW_BLOCK = 8
+BY_MATMUL = 3
+QUAD = 32
 
 FLOPS = 2 * 2 * IMAGES * PIXELS * C * C
 
@@ -56,12 +55,13 @@ def tile_hydraattention_pb_t_kernel(
         const = stack.enter_context(tc.tile_pool(name="const", bufs=1))
         x_pool = stack.enter_context(tc.tile_pool(name="x_pool", bufs=GROUPS))
         stream2 = stack.enter_context(tc.tile_pool(name="stream2", bufs=2))
+        ahead = stack.enter_context(tc.tile_pool(name="ahead", bufs=AHEAD))
         stream3 = stack.enter_context(tc.tile_pool(name="stream3", bufs=3))
-        blends = stack.enter_context(tc.tile_pool(name="blends", bufs=BLEND_LEAD + 2))
-        small = stack.enter_context(tc.tile_pool(name="small", bufs=4))
+        stream4 = stack.enter_context(tc.tile_pool(name="stream4", bufs=4))
+        stream5 = stack.enter_context(tc.tile_pool(name="stream5", bufs=5))
         psum_q = stack.enter_context(tc.psum_pool(name="psum_q", bufs=2))
-        psum_t = stack.enter_context(tc.psum_pool(name="psum_t", bufs=3))
-        psum_g = stack.enter_context(tc.psum_pool(name="psum_g", bufs=1))
+        psum_t = stack.enter_context(tc.psum_pool(name="psum_t", bufs=2))
+        psum_f = stack.enter_context(tc.psum_pool(name="psum_f", bufs=2))
         psum_y = stack.enter_context(tc.psum_pool(name="psum_y", bufs=2))
 
         warm = const.tile([P, 2], F32, name="warm")
@@ -71,7 +71,8 @@ def tile_hydraattention_pb_t_kernel(
         rows_in = const.tile([P, P], BF16, name="rows_in")
         nc.vector.memset(rows_in[:], 0.0)
         nc.sync.dma_start(out=rows_in[0:64, :], in_=mask.rearrange("b o (r a) w -> (b o r) (a w)", a=2))
-        nc.sync.dma_start(out=rows_in[64:68, :], in_=b_q.rearrange("(j m) -> j m", m=P))
+        bq = const.tile([P, BLOCKS], BF16, name="bq")
+        nc.scalar.dma_start(out=bq[:], in_=b_q.rearrange("(p t) -> p t", t=BLOCKS))
         x_raw = []
         for g in range(GROUPS):
             image, part = divmod(g, GROUPS_PER_IMAGE)
@@ -80,94 +81,89 @@ def tile_hydraattention_pb_t_kernel(
             rows = x[image].rearrange("(p t) h w -> p t (h w)", t=PACK)
             nc.sync.dma_start(out=raw[:], in_=rows[:, :, part * GROUP : (part + 1) * GROUP])
             if g == 0:
-                wq_codes, wq_plane = load_weight(nc, const, W_q_words, W_q_scales, "wq")
+                wq_raw_codes, wq_raw_plane = load_weight(nc, const, W_q_words, W_q_scales, "wq_raw")
             if g == 1:
                 wo_codes, wo_plane = load_weight(nc, const, W_out_words, W_out_scales, "wo")
 
-        know_rows, mask_rows = [], []
+        know_raw, mask_raw, piece_raw = [], [], []
         for image in range(IMAGES):
-            kk = const.tile([P, C], BF16, name="know_rows%d" % image)
-            km = const.tile([P, C], BF16, name="mask_rows%d" % image)
+            kk = const.tile([P, C], BF16, name="know_raw%d" % image)
+            km = const.tile([P, C], BF16, name="mask_raw%d" % image)
+            pr = const.tile([P, C], BF16, name="piece_raw%d" % image)
             queue = nc.scalar if image == 0 else nc.sync
             queue.dma_start(out=kk[:], in_=kv_know[image, 0, :].partition_broadcast(P))
             queue.dma_start(out=km[:], in_=kv_mask[image, 0, :].partition_broadcast(P))
-            know_rows.append(kk)
-            mask_rows.append(km)
+            for i in range(BY_MATMUL):
+                r = QUAD * i
+                queue.dma_start(out=pr[r : r + PIECES, :], in_=kv_know[image, 0, :].partition_broadcast(PIECES))
+                queue.dma_start(out=pr[r + PIECES : r + 2 * PIECES, :], in_=kv_mask[image, 0, :].partition_broadcast(PIECES))
+            know_raw.append(kk)
+            mask_raw.append(km)
+            piece_raw.append(pr)
         bo_rows = const.tile([P, C], BF16, name="bo_rows")
         nc.scalar.dma_start(out=bo_rows[:], in_=b_out.partition_broadcast(P))
-
-        vector_rows = []
-        for image in range(IMAGES):
-            vr = const.tile([P, C], BF16, name="vector_rows%d" % image)
-            nc.vector.memset(vr[:], 0.0)
-            queue = nc.scalar if image == 0 else nc.sync
-            queue.dma_start(out=vr[0:1, :], in_=kv_know[image, 0:1, :])
-            queue.dma_start(out=vr[1 : 1 + PIECES, :], in_=kv_mask[image, 0, :].partition_broadcast(PIECES))
-            queue.dma_start(out=vr[1 + PIECES : 1 + 2 * PIECES, :], in_=kv_know[image, 0, :].partition_broadcast(PIECES))
-            vector_rows.append(vr)
-        factors = const.tile([P, BY_TENSOR, P], BF16, name="factors")
-        nc.vector.memset(factors[:].rearrange("p n r -> p (n r)").bitcast(I32), 0)
 
         ident_bf16 = const.tile([P, P], BF16, name="ident_bf16")
         make_identity(nc, ident_bf16[:])
         ident_f32 = const.tile([P, P], F32, name="ident_f32")
         make_identity(nc, ident_f32[:])
 
-        cols_ps = psum_g.tile([P, P], BF16, name="cols_ps", tag="g_cp")
-        nc.tensor.transpose(cols_ps[:], rows_in[:], ident_bf16[:])
-        cols = const.tile([P, P], F32, name="cols")
-        nc.vector.tensor_copy(out=cols[:], in_=cols_ps[:])
-        m = cols[:, 0:ALL_TILES]
-        bq = cols[:, ALL_TILES : ALL_TILES + BLOCKS]
-
-        def per_pixel(label):
-            return const.tile([P, ALL_TILES], F32, name=label)
-
-        inv = per_pixel("inv")
-        nc.vector.tensor_scalar(out=inv[:], in0=m, scalar1=-1.0, scalar2=1.0, op0=ALU.mult, op1=ALU.add)
-        mixed = per_pixel("mixed")
-        nc.vector.scalar_tensor_tensor(out=mixed[:], in0=m, scalar=0.3, in1=inv[:], op0=ALU.mult, op1=ALU.add)
-        w_know = per_pixel("w_know")
-        nc.vector.tensor_tensor(out=w_know[:], in0=mixed[:], in1=inv[:], op=ALU.mult)
-        w_mask = per_pixel("w_mask")
-        nc.vector.scalar_tensor_tensor(out=w_mask[:], in0=m, scalar=0.7, in1=m, op0=ALU.mult, op1=ALU.mult)
-        w_sum = per_pixel("w_sum")
-        nc.vector.tensor_tensor(out=w_sum[:], in0=w_know[:], in1=w_mask[:], op=ALU.add)
-        r_sum = per_pixel("r_sum")
-        nc.vector.reciprocal(out=r_sum[:], in_=w_sum[:])
-        share = per_pixel("share")
-        nc.vector.tensor_tensor(out=share[:], in0=w_mask[:], in1=r_sum[:], op=ALU.mult)
-        r_sum2 = per_pixel("r_sum2")
-        nc.vector.tensor_tensor(out=r_sum2[:], in0=r_sum[:], in1=r_sum[:], op=ALU.mult)
-
-        nc.vector.memset(factors[:, :, 0], 1.0)
-        rest = share[:, EVERY - 1 : ALL_TILES : EVERY]
-        for r in range(PIECES):
-            nc.vector.tensor_copy(out=factors[:, :, 1 + r], in_=rest)
-            nc.vector.tensor_scalar(
-                out=factors[:, :, 1 + PIECES + r], in0=factors[:, :, 1 + r], scalar1=-1.0, scalar2=0.0, op0=ALU.mult, op1=ALU.add
-            )
-            if r < PIECES - 1:
-                left = const.tile([P, BY_TENSOR], F32, name="left%d" % r)
-                nc.vector.tensor_tensor(out=left[:], in0=rest, in1=factors[:, :, 1 + r], op=ALU.subtract)
-                rest = left[:]
-        factor_rows = const.tile([P, BY_TENSOR, P], BF16, name="factor_rows")
-
-        diff_rows = []
+        know_rows, mask_rows, piece_vectors = [], [], []
         for image in range(IMAGES):
-            diff = const.tile([P, C], F32, name="diff_rows%d" % image)
-            nc.vector.tensor_tensor(out=diff[:], in0=mask_rows[image][:], in1=know_rows[image][:], op=ALU.subtract)
-            diff_rows.append(diff)
+            know_rows.append(const.tile([P, C], BF16, name="know_rows%d" % image))
+            mask_rows.append(const.tile([P, C], BF16, name="mask_rows%d" % image))
+            pv = const.tile([P, BY_MATMUL, C], BF16, name="piece_vectors%d" % image)
+            nc.gpsimd.memset(pv[:].rearrange("p i c -> p (i c)").bitcast(I32), 0)
+            piece_vectors.append(pv)
+        factors = []
+        for k in range(3):
+            fk = const.tile([P, P], BF16, name="factors%d" % k)
+            nc.gpsimd.memset(fk[:].bitcast(I32), 0)
+            factors.append(fk)
 
-        x_grouped, x_quant, q_acc, q_cp, q_pp, norm2, scale = {}, {}, {}, {}, {}, {}, {}
-        blend, g_pp, g_cp, g_grouped, g_quant, y_acc, y_sb = {}, {}, {}, {}, {}, {}, {}
-        rows_ps, blend_ps = {}, {}
+        def permute(out, in_):
+            nc.gpsimd.tensor_scalar(
+                out=out.rearrange("p (t m) -> p t m", t=PACK), in0=in_.rearrange("p (m t) -> p t m", t=PACK),
+                scalar1=1.0, scalar2=0.0, op0=ALU.mult, op1=ALU.add,
+            )
 
-        def by_tensor(t):
-            return is_tile(t) and t % EVERY == EVERY - 1
+        def permute_vectors(image):
+            for i in range(BY_MATMUL):
+                rows = slice(QUAD * i, QUAD * i + 2 * PIECES)
+                permute(piece_vectors[image][rows, i, :], piece_raw[image][rows, :])
+            permute(know_rows[image][:], know_raw[image][:])
+            permute(mask_rows[image][:], mask_raw[image][:])
 
-        def starts_rows(t):
-            return is_tile(t) and t % (EVERY * ROW_BLOCK) == 0
+        permute_vectors(0)
+
+        cols_ps = psum_f.tile([P, P], BF16, name="cols_ps", tag="fac")
+        nc.tensor.transpose(cols_ps[:], rows_in[:], ident_bf16[:])
+        cols = const.tile([P, ALL_TILES], F32, name="cols")
+        nc.vector.tensor_copy(out=cols[:], in_=cols_ps[:, 0:ALL_TILES])
+        m = cols[:]
+        inv = const.tile([P, ALL_TILES], F32, name="inv")
+        nc.vector.tensor_scalar(out=inv[:], in0=m, scalar1=-1.0, scalar2=1.0, op0=ALU.mult, op1=ALU.add)
+        mixed = const.tile([P, ALL_TILES], F32, name="mixed")
+        nc.vector.scalar_tensor_tensor(out=mixed[:], in0=m, scalar=0.3, in1=inv[:], op0=ALU.mult, op1=ALU.add)
+        gates = const.tile([P, 2, ALL_TILES], F32, name="gates")
+        nc.vector.tensor_tensor(out=gates[:, 0, :], in0=mixed[:], in1=inv[:], op=ALU.mult)
+        nc.vector.scalar_tensor_tensor(out=gates[:, 1, :], in0=m, scalar=0.7, in1=m, op0=ALU.mult, op1=ALU.mult)
+
+        wq_codes = const.tile([P, C], U32, name="wq_codes", align_bytes=64)
+        wq_plane = const.tile([P, C], U8, name="wq_plane", align_bytes=64)
+
+        def permute_weight():
+            nc.vector.tensor_copy(
+                out=wq_codes[:].bitcast(I32).rearrange("p (t m) -> p t m", t=PACK),
+                in_=wq_raw_codes[:].bitcast(I32).rearrange("p (m t) -> p t m", t=PACK),
+            )
+            nc.vector.tensor_copy(
+                out=wq_plane[:].rearrange("p (t m) -> p m t", t=PACK),
+                in_=wq_raw_plane[:].rearrange("p (m t) -> p m t", t=PACK),
+            )
+
+        x_grouped, x_quant, q_acc, q_cp, q_pp, norm2, inv_norm, ab = {}, {}, {}, {}, {}, {}, {}, {}
+        rows_ps, factor_rows, scaled, fac, g_grouped, g_quant, y_acc, y_sb = {}, {}, {}, {}, {}, {}, {}, {}
 
         def is_tile(t):
             return 0 <= t < ALL_TILES
@@ -177,7 +173,7 @@ def tile_hydraattention_pb_t_kernel(
                 return
             g, i = divmod(t, TILES_PER_GROUP)
             if i == 0:
-                x_grouped[g] = stream2.tile([P, GROUP, PACK], BF16, name="x_grouped", align_bytes=64)
+                x_grouped[g] = ahead.tile([P, GROUP, PACK], BF16, name="x_grouped", align_bytes=64)
             pixels = slice(i * P, (i + 1) * P)
             if g < VECTOR_GROUPS:
                 nc.vector.tensor_copy(
@@ -196,8 +192,8 @@ def tile_hydraattention_pb_t_kernel(
                 return
             g, i = divmod(t, TILES_PER_GROUP)
             if i == 0:
-                codes = stream2.tile([P, GROUP], U32, name="x_codes", align_bytes=64)
-                plane = stream2.tile([P, GROUP], U8, name="x_plane", align_bytes=64)
+                codes = ahead.tile([P, GROUP], U32, name="x_codes", align_bytes=64)
+                plane = ahead.tile([P, GROUP], U8, name="x_plane", align_bytes=64)
                 x_quant[g] = (codes, plane)
             codes, plane = x_quant[g]
             pixels = slice(i * P, (i + 2) * P)
@@ -228,7 +224,7 @@ def tile_hydraattention_pb_t_kernel(
                 return
             g, j = divmod(b, BLOCKS)
             if j == 0:
-                q_cp[g] = stream3.tile([P, BLOCKS, GROUP], F32, name="q_cp")
+                q_cp[g] = stream5.tile([P, BLOCKS, GROUP], F32, name="q_cp")
             nc.scalar.activation(
                 out=q_cp[g][:, j, :], in_=q_acc.pop(b)[:], func=ACT.Identity, bias=bq[:, j : j + 1], scale=1.0
             )
@@ -244,80 +240,97 @@ def tile_hydraattention_pb_t_kernel(
         def sum_squares(t):
             if not is_tile(t):
                 return
+            g, i = divmod(t, TILES_PER_GROUP)
+            if i == 0:
+                norm2[g] = stream4.tile([P, TILES_PER_GROUP], F32, name="norm2")
             squares = stream3.tile([P, C], BF16, name="squares")
-            norm2[t] = small.tile([P, 1], F32, name="norm2")
-            nc.scalar.activation(out=squares[:], in_=q_pp[t][:], func=ACT.Square, accum_out=norm2[t][:])
+            nc.scalar.activation(out=squares[:], in_=q_pp.pop(t)[:], func=ACT.Square, accum_out=norm2[g][:, i : i + 1])
 
         def root(t):
             if not is_tile(t):
                 return
-            scale[t] = small.tile([P, 1], F32, name="scale")
-            nc.scalar.activation(
-                out=scale[t][:], in_=norm2.pop(t)[:], func=ACT.Abs_reciprocal_sqrt, scale=r_sum2[:, t : t + 1]
-            )
-
-        def blend_vectors(t):
-            if not is_tile(t) or by_tensor(t):
+            g, i = divmod(t, TILES_PER_GROUP)
+            if i == BY_MATMUL - 1:
+                inv_norm[g] = stream4.tile([P, TILES_PER_GROUP], F32, name="inv_norm")
+                tiles = slice(0, BY_MATMUL)
+            elif i == BY_MATMUL:
+                tiles = slice(BY_MATMUL, BY_MATMUL + 1)
+            else:
                 return
-            image = t // TILES_PER_IMAGE
-            blend[t] = blends.tile([P, C], F32, name="blend")
-            nc.vector.scalar_tensor_tensor(
-                out=blend[t][:], in0=diff_rows[image][:], scalar=share[:, t : t + 1], in1=know_rows[image][:],
-                op0=ALU.mult, op1=ALU.add,
-            )
+            nc.scalar.activation(out=inv_norm[g][:, tiles], in_=norm2[g][:, tiles], func=ACT.Abs_reciprocal_sqrt)
 
-        def transpose_factors(t):
-            if not starts_rows(t):
+        def factor_pieces(t):
+            if not is_tile(t):
                 return
-            first = t // EVERY
-            rows_ps[t] = psum_y.tile([P, ROW_BLOCK, P], BF16, name="rows_ps", tag="y_acc")
-            for i in range(ROW_BLOCK):
-                nc.tensor.transpose(rows_ps[t][:, i, :], factors[:, first + i, :], ident_bf16[:])
+            g, i = divmod(t, TILES_PER_GROUP)
+            first = g * TILES_PER_GROUP
+            if i == BY_MATMUL - 1:
+                ab[g] = stream4.tile([P, 2, TILES_PER_GROUP], F32, name="ab")
+                exact = ab[g][:, :, 0:BY_MATMUL]
+                nc.vector.tensor_tensor(
+                    out=exact, in0=gates[:, :, first : first + BY_MATMUL],
+                    in1=inv_norm[g][:, 0:BY_MATMUL].unsqueeze(1).broadcast_to([P, 2, BY_MATMUL]), op=ALU.mult,
+                )
+                fk = factors[g % 3]
+                live = fk[:].rearrange("p (i c) -> p i c", c=QUAD)[:, 0:BY_MATMUL, 0 : 2 * PIECES]
+                pieces = live.rearrange("p i (v r) -> p v i r", r=PIECES)
+                rest = stream4.tile([P, 2, BY_MATMUL], F32, name="rest")
+                nc.vector.tensor_copy(out=pieces[:, :, :, 0], in_=exact)
+                nc.vector.tensor_tensor(out=rest[:], in0=exact, in1=pieces[:, :, :, 0], op=ALU.subtract)
+                nc.vector.tensor_copy(out=pieces[:, :, :, 1], in_=rest[:])
+                nc.vector.tensor_tensor(out=pieces[:, :, :, 2], in0=rest[:], in1=pieces[:, :, :, 1], op=ALU.subtract)
+            elif i == BY_MATMUL:
+                nc.vector.tensor_tensor(
+                    out=ab[g][:, :, i : i + 1], in0=gates[:, :, t : t + 1],
+                    in1=inv_norm[g][:, i : i + 1].unsqueeze(1).broadcast_to([P, 2, 1]), op=ALU.mult,
+                )
 
-        def copy_factors(t):
-            if not starts_rows(t):
-                return
-            first = t // EVERY
-            nc.vector.tensor_copy(out=factor_rows[:, first : first + ROW_BLOCK, :], in_=rows_ps.pop(t)[:])
+        def transpose_factors(g):
+            rows_ps[g] = psum_y.tile([P, P], BF16, name="rows_ps", tag="y_acc")
+            nc.tensor.transpose(rows_ps[g][:], factors[g % 3][:], ident_bf16[:])
 
-        def blend_matmul(t):
-            if not by_tensor(t):
-                return
-            blend_ps[t] = psum_y.tile([P, C], F32, name="blend_ps", tag="y_acc")
-            nc.tensor.matmul(
-                out=blend_ps[t][:], lhsT=factor_rows[:, t // EVERY, :], rhs=vector_rows[t // TILES_PER_IMAGE][:], start=True, stop=True
-            )
+        def copy_factors(g):
+            factor_rows[g] = stream2.tile([P, P], BF16, name="factor_rows")
+            nc.scalar.copy(out=factor_rows[g][:], in_=rows_ps.pop(g)[:])
 
-        def copy_blend(t):
-            if not by_tensor(t):
+        def scale_vector(g, v):
+            if v == 0:
+                scaled[g] = stream2.tile([P, 2, C], F32, name="scaled")
+            rows = (know_rows, mask_rows)[v][g // GROUPS_PER_IMAGE]
+            nc.scalar.activation(out=scaled[g][:, v, :], in_=rows[:], func=ACT.Copy, scale=ab[g][:, v, BY_MATMUL : BY_MATMUL + 1])
+
+        def make_factor(t):
+            if not is_tile(t):
                 return
-            blend[t] = blends.tile([P, C], F32, name="blend")
-            nc.scalar.copy(out=blend[t][:], in_=blend_ps.pop(t)[:])
+            g, i = divmod(t, TILES_PER_GROUP)
+            fac[t] = psum_f.tile([P, BLOCKS, P], F32, name="fac")
+            for j in range(BLOCKS):
+                block = slice(j * P, (j + 1) * P)
+                if i < BY_MATMUL:
+                    nc.tensor.matmul(
+                        out=fac[t][:, j, :], lhsT=piece_vectors[g // GROUPS_PER_IMAGE][:, i, block], rhs=factor_rows[g][:],
+                        start=True, stop=True,
+                    )
+                else:
+                    for v in range(2):
+                        nc.tensor.matmul(
+                            out=fac[t][:, j, :], lhsT=scaled[g][:, v, block], rhs=ident_f32[:],
+                            is_transpose=True, start=(v == 0), stop=(v == 1),
+                        )
 
         def gate(t):
             if not is_tile(t):
                 return
-            g_pp[t] = stream3.tile([P, C], BF16, name="g_pp")
-            nc.vector.scalar_tensor_tensor(
-                out=g_pp[t][:], in0=q_pp.pop(t)[:], scalar=scale.pop(t)[:], in1=blend.pop(t)[:], op0=ALU.mult, op1=ALU.mult
-            )
-
-        def transpose_g(t):
-            if not is_tile(t):
-                return
+            g, i = divmod(t, TILES_PER_GROUP)
             pair, half = divmod(t, 2)
             if half == 0:
-                g_cp[pair] = psum_g.tile([P, 2, 2, P], F32, name="g_cp")
-            words = g_pp.pop(t)[:].bitcast(F32)
-            for u in range(2):
-                nc.tensor.transpose(g_cp[pair][:, half, u, :], words[:, u : C // 2 : 2], ident_f32[:])
-
-        def regroup_g(t):
-            if not is_tile(t) or t % 2 == 0:
-                return
-            pair = t // 2
-            g_grouped[pair] = stream3.tile([P, 2, P, PACK], BF16, name="g_grouped", align_bytes=64)
-            nc.scalar.copy(out=g_grouped[pair][:].bitcast(F32), in_=g_cp.pop(pair)[:].rearrange("p i u w -> p i w u"))
+                g_grouped[pair] = stream3.tile([P, 2, P, PACK], BF16, name="g_grouped", align_bytes=64)
+            nc.vector.tensor_tensor(
+                out=g_grouped[pair][:, half, :, :],
+                in0=fac.pop(t)[:].rearrange("p t w -> p w t"),
+                in1=q_cp[g][:, :, i * P : (i + 1) * P].rearrange("p t w -> p w t"),
+                op=ALU.mult,
+            )
 
         def quantise_g(t):
             if not is_tile(t) or t % 2 == 0:
@@ -361,24 +374,36 @@ def tile_hydraattention_pb_t_kernel(
                 rows = out.flatten_outer_dims()[pair * 2 * P : (pair + 1) * 2 * P, :]
                 nc.sync.dma_start(out=rows.rearrange("(i p) c -> p i c", p=P), in_=y_sb.pop(pair)[:])
 
-        for s in range(-BLEND_LEAD - 4, ALL_TILES + 6 + 1):
+        def of_group(step, lag):
+            g, i = divmod(step - lag, TILES_PER_GROUP)
+            return g if i == 0 and 0 <= g < GROUPS else None
+
+        for s in range(-11, ALL_TILES + 13):
             transpose_q(s)
-            transpose_g(s - 2)
+            g = of_group(s, 6)
+            if g is not None:
+                transpose_factors(g)
+            make_factor(s - 7)
             project_q(s + 5)
-            project_out(s - 5)
-            blend_matmul(s + BLEND_LEAD + 1)
-            transpose_factors(s + BLEND_LEAD + 4)
+            project_out(s - 11)
 
             add_bq(s + 4)
-            copy_blend(s + BLEND_LEAD)
-            copy_factors(s + BLEND_LEAD + 3)
             sum_squares(s)
-            regroup_g(s - 2)
-            regroup_x(s + 10)
             root(s)
+            if g is not None:
+                copy_factors(g)
+            for v in range(2):
+                g = of_group(s, 6 + v)
+                if g is not None:
+                    scale_vector(g, v)
+            regroup_x(s + 11)
 
-            gate(s - 1)
-            add_bo_and_store(s - 6)
-            blend_vectors(s + BLEND_LEAD)
-            quantise_g(s - 3)
-            quantise_x(s + 8)
+            factor_pieces(s - 1)
+            gate(s - 8)
+            add_bo_and_store(s - 12)
+            quantise_g(s - 9)
+            quantise_x(s + 9)
+            if s == -9:
+                permute_weight()
+            if s == 8:
+                permute_vectors(1)

@@ -326,9 +326,9 @@ def tile_hydraattention_pb_t_kernel(
             if half == 0:
                 g_grouped[pair] = stream3.tile([P, 2, P, PACK], BF16, name="g_grouped", align_bytes=64)
             nc.vector.tensor_tensor(
-                out=g_grouped[pair][:, half, :, :],
-                in0=fac.pop(t)[:].rearrange("p t w -> p w t"),
-                in1=q_cp[g][:, :, i * P : (i + 1) * P].rearrange("p t w -> p w t"),
+                out=g_grouped[pair][:, half, :, :].rearrange("p (c i) t -> p c t i", i=RUN),
+                in0=fac.pop(t)[:].rearrange("p t (c i) -> p c t i", i=RUN),
+                in1=q_cp[g][:, :, i * P : (i + 1) * P].rearrange("p t (c i) -> p c t i", i=RUN),
                 op=ALU.mult,
             )
 

@@ -24,11 +24,12 @@ GROUPS_PER_IMAGE = PIXELS // GROUP
 GROUPS = IMAGES * GROUPS_PER_IMAGE
 ALL_TILES = GROUPS * TILES_PER_GROUP
 TILES_PER_IMAGE = ALL_TILES // IMAGES
-AHEAD = 5
+AHEAD = 7
 RUN = 4
-VECTOR_GROUPS = 8
+VECTOR_GROUPS = 4
 PIECES = 3
-BY_MATMUL = 3
+VECTOR_ADDS = (4, 6, 8, 10)
+FULL_GROUPS = (0, 5, 10)
 QUAD = 32
 
 FLOPS = 2 * 2 * IMAGES * PIXELS * C * C
@@ -73,6 +74,16 @@ def tile_hydraattention_pb_t_kernel(
         nc.sync.dma_start(out=rows_in[0:64, :], in_=mask.rearrange("b o (r a) w -> (b o r) (a w)", a=2))
         bq = const.tile([P, BLOCKS], BF16, name="bq")
         nc.scalar.dma_start(out=bq[:], in_=b_q.rearrange("(p t) -> p t", t=BLOCKS))
+        know_raw, mask_raw = [], []
+        for image in range(IMAGES):
+            know_raw.append(const.tile([P, C], BF16, name="know_raw%d" % image))
+            mask_raw.append(const.tile([P, C], BF16, name="mask_raw%d" % image))
+
+        def load_rows(queue, image):
+            queue.dma_start(out=know_raw[image][:], in_=kv_know[image, 0, :].partition_broadcast(P))
+            queue.dma_start(out=mask_raw[image][:], in_=kv_mask[image, 0, :].partition_broadcast(P))
+
+        load_rows(nc.scalar, 0)
         x_raw = []
         for g in range(GROUPS):
             image, part = divmod(g, GROUPS_PER_IMAGE)
@@ -82,26 +93,14 @@ def tile_hydraattention_pb_t_kernel(
             nc.sync.dma_start(out=raw[:], in_=rows[:, :, part * GROUP : (part + 1) * GROUP])
             if g == 0:
                 wq_raw_codes, wq_raw_plane = load_weight(nc, const, W_q_words, W_q_scales, "wq_raw")
-            if g == 1:
+            if g == 3:
                 wo_codes, wo_plane = load_weight(nc, const, W_out_words, W_out_scales, "wo")
-
-        know_raw, mask_raw, piece_raw = [], [], []
-        for image in range(IMAGES):
-            kk = const.tile([P, C], BF16, name="know_raw%d" % image)
-            km = const.tile([P, C], BF16, name="mask_raw%d" % image)
-            pr = const.tile([P, C], BF16, name="piece_raw%d" % image)
-            queue = nc.scalar if image == 0 else nc.sync
-            queue.dma_start(out=kk[:], in_=kv_know[image, 0, :].partition_broadcast(P))
-            queue.dma_start(out=km[:], in_=kv_mask[image, 0, :].partition_broadcast(P))
-            for i in range(BY_MATMUL):
-                r = QUAD * i
-                queue.dma_start(out=pr[r : r + PIECES, :], in_=kv_know[image, 0, :].partition_broadcast(PIECES))
-                queue.dma_start(out=pr[r + PIECES : r + 2 * PIECES, :], in_=kv_mask[image, 0, :].partition_broadcast(PIECES))
-            know_raw.append(kk)
-            mask_raw.append(km)
-            piece_raw.append(pr)
+        load_rows(nc.sync, 1)
         bo_rows = const.tile([P, C], BF16, name="bo_rows")
         nc.scalar.dma_start(out=bo_rows[:], in_=b_out.partition_broadcast(P))
+
+        bq_f32 = const.tile([P, BLOCKS], F32, name="bq_f32")
+        nc.vector.tensor_copy(out=bq_f32[:], in_=bq[:])
 
         ident_bf16 = const.tile([P, P], BF16, name="ident_bf16")
         make_identity(nc, ident_bf16[:])
@@ -112,7 +111,7 @@ def tile_hydraattention_pb_t_kernel(
         for image in range(IMAGES):
             know_rows.append(const.tile([P, C], BF16, name="know_rows%d" % image))
             mask_rows.append(const.tile([P, C], BF16, name="mask_rows%d" % image))
-            pv = const.tile([P, BY_MATMUL, C], BF16, name="piece_vectors%d" % image)
+            pv = const.tile([P, TILES_PER_GROUP, C], BF16, name="piece_vectors%d" % image)
             nc.gpsimd.memset(pv[:].rearrange("p i c -> p (i c)").bitcast(I32), 0)
             piece_vectors.append(pv)
         factors = []
@@ -121,6 +120,9 @@ def tile_hydraattention_pb_t_kernel(
             nc.gpsimd.memset(fk[:].bitcast(I32), 0)
             factors.append(fk)
 
+        def by_matmul(g):
+            return TILES_PER_GROUP if g in FULL_GROUPS else TILES_PER_GROUP - 1
+
         def permute(out, in_):
             nc.gpsimd.tensor_scalar(
                 out=out.rearrange("p (t m) -> p t m", t=PACK), in0=in_.rearrange("p (m t) -> p t m", t=PACK),
@@ -128,9 +130,10 @@ def tile_hydraattention_pb_t_kernel(
             )
 
         def permute_vectors(image):
-            for i in range(BY_MATMUL):
-                rows = slice(QUAD * i, QUAD * i + 2 * PIECES)
-                permute(piece_vectors[image][rows, i, :], piece_raw[image][rows, :])
+            for i in range(TILES_PER_GROUP):
+                for vector, rows in ((mask_raw, 2 * PIECES), (know_raw, PIECES)):
+                    live = slice(QUAD * i, QUAD * i + rows)
+                    permute(piece_vectors[image][live, i, :], vector[image][live, :])
             permute(know_rows[image][:], know_raw[image][:])
             permute(mask_rows[image][:], mask_raw[image][:])
 
@@ -163,7 +166,7 @@ def tile_hydraattention_pb_t_kernel(
             )
 
         x_grouped, x_quant, q_acc, q_cp, q_pp, norm2, inv_norm, ab = {}, {}, {}, {}, {}, {}, {}, {}
-        rows_ps, factor_rows, scaled, fac, g_grouped, g_quant, y_acc, y_sb = {}, {}, {}, {}, {}, {}, {}, {}
+        rest, rows_ps, factor_rows, scaled, fac, g_grouped, g_quant, y_acc, y_sb = {}, {}, {}, {}, {}, {}, {}, {}, {}
 
         def is_tile(t):
             return 0 <= t < ALL_TILES
@@ -225,9 +228,14 @@ def tile_hydraattention_pb_t_kernel(
             g, j = divmod(b, BLOCKS)
             if j == 0:
                 q_cp[g] = stream5.tile([P, BLOCKS, GROUP], F32, name="q_cp")
-            nc.scalar.activation(
-                out=q_cp[g][:, j, :], in_=q_acc.pop(b)[:], func=ACT.Identity, bias=bq[:, j : j + 1], scale=1.0
-            )
+            if b in VECTOR_ADDS:
+                nc.vector.tensor_scalar(
+                    out=q_cp[g][:, j, :], in0=q_acc.pop(b)[:], scalar1=bq_f32[:, j : j + 1], scalar2=0.0, op0=ALU.add, op1=ALU.add
+                )
+            else:
+                nc.scalar.activation(
+                    out=q_cp[g][:, j, :], in_=q_acc.pop(b)[:], func=ACT.Identity, bias=bq_f32[:, j : j + 1], scale=1.0
+                )
 
         def transpose_q(t):
             if not is_tile(t):
@@ -250,36 +258,39 @@ def tile_hydraattention_pb_t_kernel(
             if not is_tile(t):
                 return
             g, i = divmod(t, TILES_PER_GROUP)
-            if i == BY_MATMUL - 1:
+            n = by_matmul(g)
+            if i == n - 1:
                 inv_norm[g] = stream4.tile([P, TILES_PER_GROUP], F32, name="inv_norm")
-                tiles = slice(0, BY_MATMUL)
-            elif i == BY_MATMUL:
-                tiles = slice(BY_MATMUL, BY_MATMUL + 1)
+                tiles = slice(0, n)
+            elif i == n:
+                tiles = slice(n, n + 1)
             else:
                 return
             nc.scalar.activation(out=inv_norm[g][:, tiles], in_=norm2[g][:, tiles], func=ACT.Abs_reciprocal_sqrt)
 
-        def factor_pieces(t):
+        def factor_pieces(t, stage):
             if not is_tile(t):
                 return
             g, i = divmod(t, TILES_PER_GROUP)
-            first = g * TILES_PER_GROUP
-            if i == BY_MATMUL - 1:
-                ab[g] = stream4.tile([P, 2, TILES_PER_GROUP], F32, name="ab")
-                exact = ab[g][:, :, 0:BY_MATMUL]
-                nc.vector.tensor_tensor(
-                    out=exact, in0=gates[:, :, first : first + BY_MATMUL],
-                    in1=inv_norm[g][:, 0:BY_MATMUL].unsqueeze(1).broadcast_to([P, 2, BY_MATMUL]), op=ALU.mult,
-                )
-                fk = factors[g % 3]
-                live = fk[:].rearrange("p (i c) -> p i c", c=QUAD)[:, 0:BY_MATMUL, 0 : 2 * PIECES]
+            n = by_matmul(g)
+            if i == n - 1:
+                live = factors[g % 3][:].rearrange("p (i c) -> p i c", c=QUAD)[:, 0:n, 0 : 2 * PIECES]
                 pieces = live.rearrange("p i (v r) -> p v i r", r=PIECES)
-                rest = stream4.tile([P, 2, BY_MATMUL], F32, name="rest")
-                nc.vector.tensor_copy(out=pieces[:, :, :, 0], in_=exact)
-                nc.vector.tensor_tensor(out=rest[:], in0=exact, in1=pieces[:, :, :, 0], op=ALU.subtract)
-                nc.vector.tensor_copy(out=pieces[:, :, :, 1], in_=rest[:])
-                nc.vector.tensor_tensor(out=pieces[:, :, :, 2], in0=rest[:], in1=pieces[:, :, :, 1], op=ALU.subtract)
-            elif i == BY_MATMUL:
+                if stage == 0:
+                    ab[g] = stream4.tile([P, 2, TILES_PER_GROUP], F32, name="ab")
+                    first = g * TILES_PER_GROUP
+                    weights = gates[:, :, first : first + n]
+                    inverse = inv_norm[g][:, 0:n].unsqueeze(1).broadcast_to([P, 2, n])
+                    nc.vector.tensor_tensor(out=ab[g][:, :, 0:n], in0=weights, in1=inverse, op=ALU.mult)
+                    nc.vector.tensor_tensor(out=pieces[:, :, :, 0], in0=weights, in1=inverse, op=ALU.mult)
+                elif stage == 1:
+                    rest[g] = stream4.tile([P, 2, n], F32, name="rest")
+                    exact = ab[g][:, :, 0:n]
+                    nc.vector.tensor_tensor(out=rest[g][:], in0=exact, in1=pieces[:, :, :, 0], op=ALU.subtract)
+                    nc.vector.tensor_tensor(out=pieces[:, :, :, 1], in0=exact, in1=pieces[:, :, :, 0], op=ALU.subtract)
+                else:
+                    nc.vector.tensor_tensor(out=pieces[:, :, :, 2], in0=rest.pop(g)[:], in1=pieces[:, :, :, 1], op=ALU.subtract)
+            elif i == n and stage == 0:
                 nc.vector.tensor_tensor(
                     out=ab[g][:, :, i : i + 1], in0=gates[:, :, t : t + 1],
                     in1=inv_norm[g][:, i : i + 1].unsqueeze(1).broadcast_to([P, 2, 1]), op=ALU.mult,
@@ -294,10 +305,12 @@ def tile_hydraattention_pb_t_kernel(
             nc.scalar.copy(out=factor_rows[g][:], in_=rows_ps.pop(g)[:])
 
         def scale_vector(g, v):
+            if by_matmul(g) == TILES_PER_GROUP:
+                return
             if v == 0:
                 scaled[g] = stream2.tile([P, 2, C], F32, name="scaled")
             rows = (know_rows, mask_rows)[v][g // GROUPS_PER_IMAGE]
-            nc.scalar.activation(out=scaled[g][:, v, :], in_=rows[:], func=ACT.Copy, scale=ab[g][:, v, BY_MATMUL : BY_MATMUL + 1])
+            nc.scalar.activation(out=scaled[g][:, v, :], in_=rows[:], func=ACT.Copy, scale=ab[g][:, v, TILES_PER_GROUP - 1 : TILES_PER_GROUP])
 
         def make_factor(t):
             if not is_tile(t):
@@ -306,7 +319,7 @@ def tile_hydraattention_pb_t_kernel(
             fac[t] = psum_f.tile([P, BLOCKS, P], F32, name="fac")
             for j in range(BLOCKS):
                 block = slice(j * P, (j + 1) * P)
-                if i < BY_MATMUL:
+                if i < by_matmul(g):
                     nc.tensor.matmul(
                         out=fac[t][:, j, :], lhsT=piece_vectors[g // GROUPS_PER_IMAGE][:, i, block], rhs=factor_rows[g][:],
                         start=True, stop=True,
@@ -378,7 +391,10 @@ def tile_hydraattention_pb_t_kernel(
             g, i = divmod(step - lag, TILES_PER_GROUP)
             return g if i == 0 and 0 <= g < GROUPS else None
 
-        for s in range(-11, ALL_TILES + 13):
+        in_order = {mybir.EngineType.PE, mybir.EngineType.Activation, mybir.EngineType.DVE}
+        stack.enter_context(tc.manual_schedule(engines=in_order))
+
+        for s in range(-16, ALL_TILES + 13):
             transpose_q(s)
             g = of_group(s, 6)
             if g is not None:
@@ -388,22 +404,33 @@ def tile_hydraattention_pb_t_kernel(
             project_out(s - 11)
 
             add_bq(s + 4)
-            sum_squares(s)
-            root(s)
             if g is not None:
                 copy_factors(g)
+            sum_squares(s)
+            root(s)
             for v in range(2):
-                g = of_group(s, 6 + v)
+                g = of_group(s, 7 + v)
                 if g is not None:
                     scale_vector(g, v)
-            regroup_x(s + 11)
 
-            factor_pieces(s - 1)
             gate(s - 8)
+            factor_pieces(s - 2, 0)
             add_bo_and_store(s - 12)
+            factor_pieces(s - 2, 1)
             quantise_g(s - 9)
-            quantise_x(s + 9)
-            if s == -9:
-                permute_weight()
+            for g in range(VECTOR_GROUPS):
+                if s == 2 * g - 7:
+                    for i in range(TILES_PER_GROUP):
+                        regroup_x(TILES_PER_GROUP * g + i)
+                    if g == 0:
+                        permute_weight()
+                    quantise_x(TILES_PER_GROUP * g)
+                    quantise_x(TILES_PER_GROUP * g + 2)
+            if s + 9 >= VECTOR_GROUPS * TILES_PER_GROUP:
+                quantise_x(s + 9)
+            factor_pieces(s - 2, 2)
+
+            if s + 16 >= VECTOR_GROUPS * TILES_PER_GROUP:
+                regroup_x(s + 16)
             if s == 8:
                 permute_vectors(1)

@@ -25,6 +25,7 @@ GROUPS = IMAGES * GROUPS_PER_IMAGE
 ALL_TILES = GROUPS * TILES_PER_GROUP
 TILES_PER_IMAGE = ALL_TILES // IMAGES
 AHEAD = 7
+GATE_RUN = 2
 RUN = 4
 VECTOR_GROUPS = 4
 PIECES = 3
@@ -339,9 +340,9 @@ def tile_hydraattention_pb_t_kernel(
             if half == 0:
                 g_grouped[pair] = stream3.tile([P, 2, P, PACK], BF16, name="g_grouped", align_bytes=64)
             nc.vector.tensor_tensor(
-                out=g_grouped[pair][:, half, :, :].rearrange("p (c i) t -> p c t i", i=RUN),
-                in0=fac.pop(t)[:].rearrange("p t (c i) -> p c t i", i=RUN),
-                in1=q_cp[g][:, :, i * P : (i + 1) * P].rearrange("p t (c i) -> p c t i", i=RUN),
+                out=g_grouped[pair][:, half, :, :].rearrange("p (c i) t -> p c t i", i=GATE_RUN),
+                in0=fac.pop(t)[:].rearrange("p t (c i) -> p c t i", i=GATE_RUN),
+                in1=q_cp[g][:, :, i * P : (i + 1) * P].rearrange("p t (c i) -> p c t i", i=GATE_RUN),
                 op=ALU.mult,
             )
 

@@ -31,6 +31,7 @@ VECTOR_GROUPS = 4
 PIECES = 3
 VECTOR_ADDS = (4, 6, 8, 10)
 FULL_GROUPS = (0, 5, 10)
+PERMUTES = 2 * TILES_PER_GROUP + 2
 QUAD = 32
 
 FLOPS = 2 * 2 * IMAGES * PIXELS * C * C
@@ -130,15 +131,19 @@ def tile_hydraattention_pb_t_kernel(
                 scalar1=1.0, scalar2=0.0, op0=ALU.mult, op1=ALU.add,
             )
 
-        def permute_vectors(image):
-            for i in range(TILES_PER_GROUP):
-                for vector, rows in ((mask_raw, 2 * PIECES), (know_raw, PIECES)):
-                    live = slice(QUAD * i, QUAD * i + rows)
-                    permute(piece_vectors[image][live, i, :], vector[image][live, :])
-            permute(know_rows[image][:], know_raw[image][:])
-            permute(mask_rows[image][:], mask_raw[image][:])
+        def permute_vectors(image, part):
+            i, over = divmod(part, 2)
+            if i < TILES_PER_GROUP:
+                vector, rows = ((mask_raw, 2 * PIECES), (know_raw, PIECES))[over]
+                live = slice(QUAD * i, QUAD * i + rows)
+                permute(piece_vectors[image][live, i, :], vector[image][live, :])
+            elif over == 0:
+                permute(know_rows[image][:], know_raw[image][:])
+            else:
+                permute(mask_rows[image][:], mask_raw[image][:])
 
-        permute_vectors(0)
+        for part in range(PERMUTES):
+            permute_vectors(0, part)
 
         cols_ps = psum_f.tile([P, P], BF16, name="cols_ps", tag="fac")
         nc.tensor.transpose(cols_ps[:], rows_in[:], ident_bf16[:])
@@ -166,7 +171,7 @@ def tile_hydraattention_pb_t_kernel(
                 in_=wq_raw_plane[:].rearrange("p (m t) -> p m t", t=PACK),
             )
 
-        x_grouped, x_quant, q_acc, q_cp, q_pp, norm2, inv_norm, ab = {}, {}, {}, {}, {}, {}, {}, {}
+        x_grouped, x_tile, x_quant, q_acc, q_cp, q_pp, norm2, inv_norm, ab = {}, {}, {}, {}, {}, {}, {}, {}, {}
         rest, rows_ps, factor_rows, scaled, fac, g_grouped, g_quant, y_acc, y_sb = {}, {}, {}, {}, {}, {}, {}, {}, {}
 
         def is_tile(t):
@@ -176,34 +181,39 @@ def tile_hydraattention_pb_t_kernel(
             if not is_tile(t):
                 return
             g, i = divmod(t, TILES_PER_GROUP)
-            if i == 0:
-                x_grouped[g] = ahead.tile([P, GROUP, PACK], BF16, name="x_grouped", align_bytes=64)
             pixels = slice(i * P, (i + 1) * P)
             if g < VECTOR_GROUPS:
+                if i == 0:
+                    x_grouped[g] = stream2.tile([P, GROUP, PACK], BF16, name="x_grouped", align_bytes=64)
                 nc.vector.tensor_copy(
                     out=x_grouped[g][:, pixels, :].rearrange("p (c i) t -> p c t i", i=RUN),
                     in_=x_raw[g][:, :, pixels].rearrange("p t (c i) -> p c t i", i=RUN),
                 )
             else:
+                x_tile[t] = stream4.tile([P, P, PACK], BF16, name="x_tile", align_bytes=64)
                 nc.gpsimd.tensor_scalar(
-                    out=x_grouped[g][:, pixels, :],
+                    out=x_tile[t][:],
                     in0=x_raw[g][:, :, pixels].rearrange("p t w -> p w t"),
                     scalar1=1.0, scalar2=0.0, op0=ALU.mult, op1=ALU.add,
                 )
 
         def quantise_x(t):
-            if not is_tile(t) or t % 2 != 0:
-                return
             g, i = divmod(t, TILES_PER_GROUP)
+            if not is_tile(t) or (g < VECTOR_GROUPS and i % 2 != 0):
+                return
             if i == 0:
                 codes = ahead.tile([P, GROUP], U32, name="x_codes", align_bytes=64)
                 plane = ahead.tile([P, GROUP], U8, name="x_plane", align_bytes=64)
                 x_quant[g] = (codes, plane)
             codes, plane = x_quant[g]
-            pixels = slice(i * P, (i + 2) * P)
+            if g < VECTOR_GROUPS:
+                pixels = slice(i * P, (i + 2) * P)
+                values = x_grouped[g][:, pixels, :]
+            else:
+                pixels = slice(i * P, (i + 1) * P)
+                values = x_tile.pop(t)[:]
             nc.vector.quantize_mx(
-                out=codes[:, pixels].bitcast(FP8X4), scales=plane[:, pixels],
-                in_=x_grouped[g][:, pixels, :].rearrange("p w t -> p (w t)"),
+                out=codes[:, pixels].bitcast(FP8X4), scales=plane[:, pixels], in_=values.rearrange("p w t -> p (w t)"),
             )
 
         def project_q(b):
@@ -392,7 +402,7 @@ def tile_hydraattention_pb_t_kernel(
             g, i = divmod(step - lag, TILES_PER_GROUP)
             return g if i == 0 and 0 <= g < GROUPS else None
 
-        in_order = {mybir.EngineType.PE, mybir.EngineType.Activation, mybir.EngineType.DVE}
+        in_order = {mybir.EngineType.PE, mybir.EngineType.Activation, mybir.EngineType.DVE, mybir.EngineType.Pool}
         stack.enter_context(tc.manual_schedule(engines=in_order))
 
         for s in range(-16, ALL_TILES + 13):
@@ -415,10 +425,11 @@ def tile_hydraattention_pb_t_kernel(
                     scale_vector(g, v)
 
             gate(s - 8)
-            factor_pieces(s - 2, 0)
             add_bo_and_store(s - 12)
-            factor_pieces(s - 2, 1)
+            factor_pieces(s - 2, 0)
             quantise_g(s - 9)
+            factor_pieces(s - 2, 1)
+            factor_pieces(s - 2, 2)
             for g in range(VECTOR_GROUPS):
                 if s == 2 * g - 7:
                     for i in range(TILES_PER_GROUP):
@@ -427,11 +438,11 @@ def tile_hydraattention_pb_t_kernel(
                         permute_weight()
                     quantise_x(TILES_PER_GROUP * g)
                     quantise_x(TILES_PER_GROUP * g + 2)
-            if s + 9 >= VECTOR_GROUPS * TILES_PER_GROUP:
-                quantise_x(s + 9)
-            factor_pieces(s - 2, 2)
+            if s + 10 >= VECTOR_GROUPS * TILES_PER_GROUP:
+                quantise_x(s + 10)
 
-            if s + 16 >= VECTOR_GROUPS * TILES_PER_GROUP:
-                regroup_x(s + 16)
-            if s == 8:
-                permute_vectors(1)
+            if s + 13 >= VECTOR_GROUPS * TILES_PER_GROUP:
+                regroup_x(s + 13)
+            part, odd = divmod(s - 18, 2)
+            if odd == 0 and 0 <= part < PERMUTES:
+                permute_vectors(1, part)

@@ -29,9 +29,7 @@ GATE_RUN = 2
 RUN = 4
 VECTOR_GROUPS = 4
 PIECES = 3
-VECTOR_ADDS = (4, 6, 8, 10)
 FULL_GROUPS = (0, 5, 10)
-PERMUTES = 2 * TILES_PER_GROUP + 2
 QUAD = 32
 
 FLOPS = 2 * 2 * IMAGES * PIXELS * C * C
@@ -76,14 +74,25 @@ def tile_hydraattention_pb_t_kernel(
         nc.sync.dma_start(out=rows_in[0:64, :], in_=mask.rearrange("b o (r a) w -> (b o r) (a w)", a=2))
         bq = const.tile([P, BLOCKS], BF16, name="bq")
         nc.scalar.dma_start(out=bq[:], in_=b_q.rearrange("(p t) -> p t", t=BLOCKS))
-        know_raw, mask_raw = [], []
+        know_rows, mask_rows, piece_vectors = [], [], []
         for image in range(IMAGES):
-            know_raw.append(const.tile([P, C], BF16, name="know_raw%d" % image))
-            mask_raw.append(const.tile([P, C], BF16, name="mask_raw%d" % image))
+            know_rows.append(const.tile([P, C], BF16, name="know_rows%d" % image))
+            mask_rows.append(const.tile([P, C], BF16, name="mask_rows%d" % image))
+            pv = const.tile([P, TILES_PER_GROUP, C], BF16, name="piece_vectors%d" % image)
+            nc.gpsimd.memset(pv[:].rearrange("p i c -> p (i c)").bitcast(I32), 0)
+            piece_vectors.append(pv)
 
         def load_rows(queue, image):
-            queue.dma_start(out=know_raw[image][:], in_=kv_know[image, 0, :].partition_broadcast(P))
-            queue.dma_start(out=mask_raw[image][:], in_=kv_mask[image, 0, :].partition_broadcast(P))
+            queue.dma_start(out=know_rows[image][:], in_=kv_know[image, 0, :].partition_broadcast(P))
+            queue.dma_start(out=mask_rows[image][:], in_=kv_mask[image, 0, :].partition_broadcast(P))
+
+        def load_piece_rows(image):
+            for i in range(TILES_PER_GROUP):
+                first = QUAD * i
+                for vector in (kv_know, kv_mask):
+                    rows = piece_vectors[image][first : first + PIECES, i, :]
+                    nc.sync.dma_start(out=rows, in_=vector[image, 0, :].partition_broadcast(PIECES))
+                    first += PIECES
 
         load_rows(nc.scalar, 0)
         x_raw = []
@@ -96,26 +105,19 @@ def tile_hydraattention_pb_t_kernel(
             if g == 0:
                 wq_raw_codes, wq_raw_plane = load_weight(nc, const, W_q_words, W_q_scales, "wq_raw")
             if g == 3:
+                load_piece_rows(0)
+            if g == 4:
                 wo_codes, wo_plane = load_weight(nc, const, W_out_words, W_out_scales, "wo")
         load_rows(nc.sync, 1)
+        load_piece_rows(1)
         bo_rows = const.tile([P, C], BF16, name="bo_rows")
         nc.scalar.dma_start(out=bo_rows[:], in_=b_out.partition_broadcast(P))
-
-        bq_f32 = const.tile([P, BLOCKS], F32, name="bq_f32")
-        nc.vector.tensor_copy(out=bq_f32[:], in_=bq[:])
 
         ident_bf16 = const.tile([P, P], BF16, name="ident_bf16")
         make_identity(nc, ident_bf16[:])
         ident_f32 = const.tile([P, P], F32, name="ident_f32")
         make_identity(nc, ident_f32[:])
 
-        know_rows, mask_rows, piece_vectors = [], [], []
-        for image in range(IMAGES):
-            know_rows.append(const.tile([P, C], BF16, name="know_rows%d" % image))
-            mask_rows.append(const.tile([P, C], BF16, name="mask_rows%d" % image))
-            pv = const.tile([P, TILES_PER_GROUP, C], BF16, name="piece_vectors%d" % image)
-            nc.gpsimd.memset(pv[:].rearrange("p i c -> p (i c)").bitcast(I32), 0)
-            piece_vectors.append(pv)
         factors = []
         for k in range(3):
             fk = const.tile([P, P], BF16, name="factors%d" % k)
@@ -124,26 +126,6 @@ def tile_hydraattention_pb_t_kernel(
 
         def by_matmul(g):
             return TILES_PER_GROUP if g in FULL_GROUPS else TILES_PER_GROUP - 1
-
-        def permute(out, in_):
-            nc.gpsimd.tensor_scalar(
-                out=out.rearrange("p (t m) -> p t m", t=PACK), in0=in_.rearrange("p (m t) -> p t m", t=PACK),
-                scalar1=1.0, scalar2=0.0, op0=ALU.mult, op1=ALU.add,
-            )
-
-        def permute_vectors(image, part):
-            i, over = divmod(part, 2)
-            if i < TILES_PER_GROUP:
-                vector, rows = ((mask_raw, 2 * PIECES), (know_raw, PIECES))[over]
-                live = slice(QUAD * i, QUAD * i + rows)
-                permute(piece_vectors[image][live, i, :], vector[image][live, :])
-            elif over == 0:
-                permute(know_rows[image][:], know_raw[image][:])
-            else:
-                permute(mask_rows[image][:], mask_raw[image][:])
-
-        for part in range(PERMUTES):
-            permute_vectors(0, part)
 
         cols_ps = psum_f.tile([P, P], BF16, name="cols_ps", tag="fac")
         nc.tensor.transpose(cols_ps[:], rows_in[:], ident_bf16[:])
@@ -239,14 +221,9 @@ def tile_hydraattention_pb_t_kernel(
             g, j = divmod(b, BLOCKS)
             if j == 0:
                 q_cp[g] = stream5.tile([P, BLOCKS, GROUP], F32, name="q_cp")
-            if b in VECTOR_ADDS:
-                nc.vector.tensor_scalar(
-                    out=q_cp[g][:, j, :], in0=q_acc.pop(b)[:], scalar1=bq_f32[:, j : j + 1], scalar2=0.0, op0=ALU.add, op1=ALU.add
-                )
-            else:
-                nc.scalar.activation(
-                    out=q_cp[g][:, j, :], in_=q_acc.pop(b)[:], func=ACT.Identity, bias=bq_f32[:, j : j + 1], scale=1.0
-                )
+            nc.scalar.activation(
+                out=q_cp[g][:, j, :], in_=q_acc.pop(b)[:], func=ACT.Identity, bias=bq[:, j : j + 1], scale=1.0
+            )
 
         def transpose_q(t):
             if not is_tile(t):
@@ -321,7 +298,10 @@ def tile_hydraattention_pb_t_kernel(
             if v == 0:
                 scaled[g] = stream2.tile([P, 2, C], F32, name="scaled")
             rows = (know_rows, mask_rows)[v][g // GROUPS_PER_IMAGE]
-            nc.scalar.activation(out=scaled[g][:, v, :], in_=rows[:], func=ACT.Copy, scale=ab[g][:, v, TILES_PER_GROUP - 1 : TILES_PER_GROUP])
+            nc.scalar.activation(
+                out=scaled[g][:, v, :].rearrange("p (t m) -> p t m", t=PACK), in_=rows[:].rearrange("p (m t) -> p t m", t=PACK),
+                func=ACT.Copy, scale=ab[g][:, v, TILES_PER_GROUP - 1 : TILES_PER_GROUP],
+            )
 
         def make_factor(t):
             if not is_tile(t):
@@ -332,7 +312,7 @@ def tile_hydraattention_pb_t_kernel(
                 block = slice(j * P, (j + 1) * P)
                 if i < by_matmul(g):
                     nc.tensor.matmul(
-                        out=fac[t][:, j, :], lhsT=piece_vectors[g // GROUPS_PER_IMAGE][:, i, block], rhs=factor_rows[g][:],
+                        out=fac[t][:, j, :], lhsT=piece_vectors[g // GROUPS_PER_IMAGE][:, i, j:C:PACK], rhs=factor_rows[g][:],
                         start=True, stop=True,
                     )
                 else:
@@ -443,6 +423,3 @@ def tile_hydraattention_pb_t_kernel(
 
             if s + 13 >= VECTOR_GROUPS * TILES_PER_GROUP:
                 regroup_x(s + 13)
-            part, odd = divmod(s - 18, 2)
-            if odd == 0 and 0 <= part < PERMUTES:
-                permute_vectors(1, part)

@@ -385,31 +385,33 @@ def tile_hydraattention_pb_t_kernel(
         in_order = {mybir.EngineType.PE, mybir.EngineType.Activation, mybir.EngineType.DVE, mybir.EngineType.Pool}
         stack.enter_context(tc.manual_schedule(engines=in_order))
 
-        for s in range(-16, ALL_TILES + 13):
-            transpose_q(s)
-            g = of_group(s, 6)
-            if g is not None:
-                transpose_factors(g)
-            make_factor(s - 7)
+        for s in range(-16, ALL_TILES + 14):
+            make_factor(s - 8)
+            if s % 2 == 0:
+                transpose_q(s)
+                transpose_q(s + 1)
+            rows_group = of_group(s, 7)
+            if rows_group is not None:
+                transpose_factors(rows_group)
             project_q(s + 5)
-            project_out(s - 11)
+            project_out(s - 12)
 
             add_bq(s + 4)
-            if g is not None:
-                copy_factors(g)
+            if rows_group is not None:
+                copy_factors(rows_group)
             sum_squares(s)
             root(s)
             for v in range(2):
-                g = of_group(s, 7 + v)
+                g = of_group(s, 8 + v)
                 if g is not None:
                     scale_vector(g, v)
 
-            gate(s - 8)
-            add_bo_and_store(s - 12)
-            factor_pieces(s - 2, 0)
-            quantise_g(s - 9)
-            factor_pieces(s - 2, 1)
+            gate(s - 9)
+            add_bo_and_store(s - 13)
             factor_pieces(s - 2, 2)
+            factor_pieces(s - 1, 0)
+            quantise_g(s - 10)
+            factor_pieces(s - 1, 1)
             for g in range(VECTOR_GROUPS):
                 if s == 2 * g - 7:
                     for i in range(TILES_PER_GROUP):

from contextlib import ExitStack

import concourse.mybir as mybir
from concourse.masks import make_identity

F32 = mybir.dt.float32
BF16 = mybir.dt.bfloat16
I32 = mybir.dt.int32
U32 = mybir.dt.uint32
U8 = mybir.dt.uint8
FP8X4 = mybir.dt.float8_e4m3fn_x4
ALU = mybir.AluOpType
ACT = mybir.ActivationFunctionType

P = 128
PACK = 4
IMAGES = 2
C = 512
PIXELS = 4096
BLOCKS = C // P
GROUP = 512
TILES_PER_GROUP = GROUP // P
GROUPS_PER_IMAGE = PIXELS // GROUP
GROUPS = IMAGES * GROUPS_PER_IMAGE
ALL_TILES = GROUPS * TILES_PER_GROUP
TILES_PER_IMAGE = ALL_TILES // IMAGES
AHEAD = 7
GATE_RUN = 2
RUN = 4
VECTOR_GROUPS = 4
PIECES = 3
FULL_GROUPS = (0, 5, 10)
QUAD = 32

FLOPS = 2 * 2 * IMAGES * PIXELS * C * C


def load_weight(nc, pool, words, scales, label):
    codes = pool.tile([P, C], U32, name=label + "_codes", align_bytes=64)
    plane = pool.tile([P, C], U8, name=label + "_plane", align_bytes=64)
    nc.vector.memset(plane[:].bitcast(I32), 0)
    nc.sync.dma_start(out=codes[:].bitcast(I32), in_=words[0].rearrange("p n t -> p (n t)").bitcast(I32))
    for quadrant in range(4):
        nc.sync.dma_start(
            out=plane[32 * quadrant : 32 * quadrant + 4, :].bitcast(I32),
            in_=scales[0, 4 * quadrant : 4 * quadrant + 4, :].bitcast(I32),
        )
    return codes, plane


def tile_hydraattention_pb_t_kernel(
    tc, x, mask, W_q_words, W_q_scales, b_q, kv_know, kv_mask, W_out_words, W_out_scales, b_out, out
):
    nc = tc.nc
    with ExitStack() as stack:
        const = stack.enter_context(tc.tile_pool(name="const", bufs=1))
        x_pool = stack.enter_context(tc.tile_pool(name="x_pool", bufs=GROUPS))
        stream2 = stack.enter_context(tc.tile_pool(name="stream2", bufs=2))
        ahead = stack.enter_context(tc.tile_pool(name="ahead", bufs=AHEAD))
        stream3 = stack.enter_context(tc.tile_pool(name="stream3", bufs=3))
        stream4 = stack.enter_context(tc.tile_pool(name="stream4", bufs=4))
        stream5 = stack.enter_context(tc.tile_pool(name="stream5", bufs=5))
        psum_q = stack.enter_context(tc.psum_pool(name="psum_q", bufs=2))
        psum_t = stack.enter_context(tc.psum_pool(name="psum_t", bufs=2))
        psum_f = stack.enter_context(tc.psum_pool(name="psum_f", bufs=2))
        psum_y = stack.enter_context(tc.psum_pool(name="psum_y", bufs=2))

        warm = const.tile([P, 2], F32, name="warm")
        nc.gpsimd.memset(warm[:], 1.0)
        nc.scalar.activation(out=warm[:, 1:2], in_=warm[:, 0:1], func=ACT.Abs_reciprocal_sqrt)

        rows_in = const.tile([P, P], BF16, name="rows_in")
        nc.vector.memset(rows_in[:], 0.0)
        nc.sync.dma_start(out=rows_in[0:64, :], in_=mask.rearrange("b o (r a) w -> (b o r) (a w)", a=2))
        bq = const.tile([P, BLOCKS], BF16, name="bq")
        nc.scalar.dma_start(out=bq[:], in_=b_q.rearrange("(p t) -> p t", t=BLOCKS))
        know_rows, mask_rows, piece_vectors = [], [], []
        for image in range(IMAGES):
            know_rows.append(const.tile([P, C], BF16, name="know_rows%d" % image))
            mask_rows.append(const.tile([P, C], BF16, name="mask_rows%d" % image))
            pv = const.tile([P, TILES_PER_GROUP, C], BF16, name="piece_vectors%d" % image)
            nc.gpsimd.memset(pv[:].rearrange("p i c -> p (i c)").bitcast(I32), 0)
            piece_vectors.append(pv)

        def load_rows(queue, image):
            queue.dma_start(out=know_rows[image][:], in_=kv_know[image, 0, :].partition_broadcast(P))
            queue.dma_start(out=mask_rows[image][:], in_=kv_mask[image, 0, :].partition_broadcast(P))

        def load_piece_rows(image):
            for i in range(TILES_PER_GROUP):
                first = QUAD * i
                for vector in (kv_know, kv_mask):
                    rows = piece_vectors[image][first : first + PIECES, i, :]
                    nc.sync.dma_start(out=rows, in_=vector[image, 0, :].partition_broadcast(PIECES))
                    first += PIECES

        load_rows(nc.scalar, 0)
        x_raw = []
        for g in range(GROUPS):
            image, part = divmod(g, GROUPS_PER_IMAGE)
            raw = x_pool.tile([P, PACK, GROUP], BF16, name="x_raw")
            x_raw.append(raw)
            rows = x[image].rearrange("(p t) h w -> p t (h w)", t=PACK)
            nc.sync.dma_start(out=raw[:], in_=rows[:, :, part * GROUP : (part + 1) * GROUP])
            if g == 0:
                wq_raw_codes, wq_raw_plane = load_weight(nc, const, W_q_words, W_q_scales, "wq_raw")
            if g == 3:
                load_piece_rows(0)
            if g == 4:
                wo_codes, wo_plane = load_weight(nc, const, W_out_words, W_out_scales, "wo")
        load_rows(nc.sync, 1)
        load_piece_rows(1)
        bo_rows = const.tile([P, C], BF16, name="bo_rows")
        nc.scalar.dma_start(out=bo_rows[:], in_=b_out.partition_broadcast(P))

        ident_bf16 = const.tile([P, P], BF16, name="ident_bf16")
        make_identity(nc, ident_bf16[:])
        ident_f32 = const.tile([P, P], F32, name="ident_f32")
        make_identity(nc, ident_f32[:])

        factors = []
        for k in range(3):
            fk = const.tile([P, P], BF16, name="factors%d" % k)
            nc.gpsimd.memset(fk[:].bitcast(I32), 0)
            factors.append(fk)

        def by_matmul(g):
            return TILES_PER_GROUP if g in FULL_GROUPS else TILES_PER_GROUP - 1

        cols_ps = psum_f.tile([P, P], BF16, name="cols_ps", tag="fac")
        nc.tensor.transpose(cols_ps[:], rows_in[:], ident_bf16[:])
        cols = const.tile([P, ALL_TILES], F32, name="cols")
        nc.vector.tensor_copy(out=cols[:], in_=cols_ps[:, 0:ALL_TILES])
        m = cols[:]
        inv = const.tile([P, ALL_TILES], F32, name="inv")
        nc.vector.tensor_scalar(out=inv[:], in0=m, scalar1=-1.0, scalar2=1.0, op0=ALU.mult, op1=ALU.add)
        mixed = const.tile([P, ALL_TILES], F32, name="mixed")
        nc.vector.scalar_tensor_tensor(out=mixed[:], in0=m, scalar=0.3, in1=inv[:], op0=ALU.mult, op1=ALU.add)
        gates = const.tile([P, 2, ALL_TILES], F32, name="gates")
        nc.vector.tensor_tensor(out=gates[:, 0, :], in0=mixed[:], in1=inv[:], op=ALU.mult)
        nc.vector.scalar_tensor_tensor(out=gates[:, 1, :], in0=m, scalar=0.7, in1=m, op0=ALU.mult, op1=ALU.mult)

        wq_codes = const.tile([P, C], U32, name="wq_codes", align_bytes=64)
        wq_plane = const.tile([P, C], U8, name="wq_plane", align_bytes=64)

        def permute_weight():
            nc.vector.tensor_copy(
                out=wq_codes[:].bitcast(I32).rearrange("p (t m) -> p t m", t=PACK),
                in_=wq_raw_codes[:].bitcast(I32).rearrange("p (m t) -> p t m", t=PACK),
            )
            nc.vector.tensor_copy(
                out=wq_plane[:].rearrange("p (t m) -> p m t", t=PACK),
                in_=wq_raw_plane[:].rearrange("p (m t) -> p m t", t=PACK),
            )

        x_grouped, x_tile, x_quant, q_acc, q_cp, q_pp, norm2, inv_norm, ab = {}, {}, {}, {}, {}, {}, {}, {}, {}
        rest, rows_ps, factor_rows, scaled, fac, g_grouped, g_quant, y_acc, y_sb = {}, {}, {}, {}, {}, {}, {}, {}, {}

        def is_tile(t):
            return 0 <= t < ALL_TILES

        def regroup_x(t):
            if not is_tile(t):
                return
            g, i = divmod(t, TILES_PER_GROUP)
            pixels = slice(i * P, (i + 1) * P)
            if g < VECTOR_GROUPS:
                if i == 0:
                    x_grouped[g] = stream2.tile([P, GROUP, PACK], BF16, name="x_grouped", align_bytes=64)
                nc.vector.tensor_copy(
                    out=x_grouped[g][:, pixels, :].rearrange("p (c i) t -> p c t i", i=RUN),
                    in_=x_raw[g][:, :, pixels].rearrange("p t (c i) -> p c t i", i=RUN),
                )
            else:
                x_tile[t] = stream4.tile([P, P, PACK], BF16, name="x_tile", align_bytes=64)
                nc.gpsimd.tensor_scalar(
                    out=x_tile[t][:],
                    in0=x_raw[g][:, :, pixels].rearrange("p t w -> p w t"),
                    scalar1=1.0, scalar2=0.0, op0=ALU.mult, op1=ALU.add,
                )

        def quantise_x(t):
            g, i = divmod(t, TILES_PER_GROUP)
            if not is_tile(t) or (g < VECTOR_GROUPS and i % 2 != 0):
                return
            if i == 0:
                codes = ahead.tile([P, GROUP], U32, name="x_codes", align_bytes=64)
                plane = ahead.tile([P, GROUP], U8, name="x_plane", align_bytes=64)
                x_quant[g] = (codes, plane)
            codes, plane = x_quant[g]
            if g < VECTOR_GROUPS:
                pixels = slice(i * P, (i + 2) * P)
                values = x_grouped[g][:, pixels, :]
            else:
                pixels = slice(i * P, (i + 1) * P)
                values = x_tile.pop(t)[:]
            nc.vector.quantize_mx(
                out=codes[:, pixels].bitcast(FP8X4), scales=plane[:, pixels], in_=values.rearrange("p w t -> p (w t)"),
            )

        def project_q(b):
            if not is_tile(b):
                return
            g, j = divmod(b, BLOCKS)
            codes, plane = x_quant[g]
            block = slice(j * P, (j + 1) * P)
            q_acc[b] = psum_q.tile([P, GROUP], F32, name="q_acc")
            nc.tensor.matmul_mx(
                out=q_acc[b][:],
                lhsT=wq_codes[:, block].bitcast(FP8X4),
                lhsT_scale=wq_plane[:, block],
                rhs=codes[:].bitcast(FP8X4),
                rhs_scale=plane[:],
                start=True,
                stop=True,
            )

        def add_bq(b):
            if not is_tile(b):
                return
            g, j = divmod(b, BLOCKS)
            if j == 0:
                q_cp[g] = stream5.tile([P, BLOCKS, GROUP], F32, name="q_cp")
            nc.scalar.activation(
                out=q_cp[g][:, j, :], in_=q_acc.pop(b)[:], func=ACT.Identity, bias=bq[:, j : j + 1], scale=1.0
            )

        def transpose_q(t):
            if not is_tile(t):
                return
            g, i = divmod(t, TILES_PER_GROUP)
            q_pp[t] = psum_t.tile([P, C], F32, name="q_pp")
            for j in range(BLOCKS):
                nc.tensor.transpose(q_pp[t][:, j * P : (j + 1) * P], q_cp[g][:, j, i * P : (i + 1) * P], ident_f32[:])

        def sum_squares(t):
            if not is_tile(t):
                return
            g, i = divmod(t, TILES_PER_GROUP)
            if i == 0:
                norm2[g] = stream4.tile([P, TILES_PER_GROUP], F32, name="norm2")
            squares = stream3.tile([P, C], BF16, name="squares")
            nc.scalar.activation(out=squares[:], in_=q_pp.pop(t)[:], func=ACT.Square, accum_out=norm2[g][:, i : i + 1])

        def root(t):
            if not is_tile(t):
                return
            g, i = divmod(t, TILES_PER_GROUP)
            n = by_matmul(g)
            if i == n - 1:
                inv_norm[g] = stream4.tile([P, TILES_PER_GROUP], F32, name="inv_norm")
                tiles = slice(0, n)
            elif i == n:
                tiles = slice(n, n + 1)
            else:
                return
            nc.scalar.activation(out=inv_norm[g][:, tiles], in_=norm2[g][:, tiles], func=ACT.Abs_reciprocal_sqrt)

        def factor_pieces(t, stage):
            if not is_tile(t):
                return
            g, i = divmod(t, TILES_PER_GROUP)
            n = by_matmul(g)
            if i == n - 1:
                live = factors[g % 3][:].rearrange("p (i c) -> p i c", c=QUAD)[:, 0:n, 0 : 2 * PIECES]
                pieces = live.rearrange("p i (v r) -> p v i r", r=PIECES)
                if stage == 0:
                    ab[g] = stream4.tile([P, 2, TILES_PER_GROUP], F32, name="ab")
                    first = g * TILES_PER_GROUP
                    weights = gates[:, :, first : first + n]
                    inverse = inv_norm[g][:, 0:n].unsqueeze(1).broadcast_to([P, 2, n])
                    nc.vector.tensor_tensor(out=ab[g][:, :, 0:n], in0=weights, in1=inverse, op=ALU.mult)
                    nc.vector.tensor_tensor(out=pieces[:, :, :, 0], in0=weights, in1=inverse, op=ALU.mult)
                elif stage == 1:
                    rest[g] = stream4.tile([P, 2, n], F32, name="rest")
                    exact = ab[g][:, :, 0:n]
                    nc.vector.tensor_tensor(out=rest[g][:], in0=exact, in1=pieces[:, :, :, 0], op=ALU.subtract)
                    nc.vector.tensor_tensor(out=pieces[:, :, :, 1], in0=exact, in1=pieces[:, :, :, 0], op=ALU.subtract)
                else:
                    nc.vector.tensor_tensor(out=pieces[:, :, :, 2], in0=rest.pop(g)[:], in1=pieces[:, :, :, 1], op=ALU.subtract)
            elif i == n and stage == 0:
                nc.vector.tensor_tensor(
                    out=ab[g][:, :, i : i + 1], in0=gates[:, :, t : t + 1],
                    in1=inv_norm[g][:, i : i + 1].unsqueeze(1).broadcast_to([P, 2, 1]), op=ALU.mult,
                )

        def transpose_factors(g):
            rows_ps[g] = psum_y.tile([P, P], BF16, name="rows_ps", tag="y_acc")
            nc.tensor.transpose(rows_ps[g][:], factors[g % 3][:], ident_bf16[:])

        def copy_factors(g):
            factor_rows[g] = stream2.tile([P, P], BF16, name="factor_rows")
            nc.scalar.copy(out=factor_rows[g][:], in_=rows_ps.pop(g)[:])

        def scale_vector(g, v):
            if by_matmul(g) == TILES_PER_GROUP:
                return
            if v == 0:
                scaled[g] = stream2.tile([P, 2, C], F32, name="scaled")
            rows = (know_rows, mask_rows)[v][g // GROUPS_PER_IMAGE]
            nc.scalar.activation(
                out=scaled[g][:, v, :].rearrange("p (t m) -> p t m", t=PACK), in_=rows[:].rearrange("p (m t) -> p t m", t=PACK),
                func=ACT.Copy, scale=ab[g][:, v, TILES_PER_GROUP - 1 : TILES_PER_GROUP],
            )

        def make_factor(t):
            if not is_tile(t):
                return
            g, i = divmod(t, TILES_PER_GROUP)
            fac[t] = psum_f.tile([P, BLOCKS, P], F32, name="fac")
            for j in range(BLOCKS):
                block = slice(j * P, (j + 1) * P)
                if i < by_matmul(g):
                    nc.tensor.matmul(
                        out=fac[t][:, j, :], lhsT=piece_vectors[g // GROUPS_PER_IMAGE][:, i, j:C:PACK], rhs=factor_rows[g][:],
                        start=True, stop=True,
                    )
                else:
                    for v in range(2):
                        nc.tensor.matmul(
                            out=fac[t][:, j, :], lhsT=scaled[g][:, v, block], rhs=ident_f32[:],
                            is_transpose=True, start=(v == 0), stop=(v == 1),
                        )

        def gate(t):
            if not is_tile(t):
                return
            g, i = divmod(t, TILES_PER_GROUP)
            pair, half = divmod(t, 2)
            if half == 0:
                g_grouped[pair] = stream3.tile([P, 2, P, PACK], BF16, name="g_grouped", align_bytes=64)
            nc.vector.tensor_tensor(
                out=g_grouped[pair][:, half, :, :].rearrange("p (c i) t -> p c t i", i=GATE_RUN),
                in0=fac.pop(t)[:].rearrange("p t (c i) -> p c t i", i=GATE_RUN),
                in1=q_cp[g][:, :, i * P : (i + 1) * P].rearrange("p t (c i) -> p c t i", i=GATE_RUN),
                op=ALU.mult,
            )

        def quantise_g(t):
            if not is_tile(t) or t % 2 == 0:
                return
            pair = t // 2
            codes = stream3.tile([P, 2 * P], U32, name="g_codes", align_bytes=64)
            plane = stream3.tile([P, 2 * P], U8, name="g_plane", align_bytes=64)
            nc.vector.quantize_mx(
                out=codes[:].bitcast(FP8X4), scales=plane[:],
                in_=g_grouped.pop(pair)[:].rearrange("p i w t -> p (i w t)"),
            )
            g_quant[pair] = (codes, plane)

        def project_out(t):
            if not is_tile(t):
                return
            pair, half = divmod(t, 2)
            codes, plane = g_quant[pair]
            pixels = slice(half * P, (half + 1) * P)
            y_acc[t] = psum_y.tile([P, C], F32, name="y_acc")
            nc.tensor.matmul_mx(
                out=y_acc[t][:],
                lhsT=codes[:, pixels].bitcast(FP8X4),
                lhsT_scale=plane[:, pixels],
                rhs=wo_codes[:].bitcast(FP8X4),
                rhs_scale=wo_plane[:],
                start=True,
                stop=True,
            )

        def add_bo_and_store(t):
            if not is_tile(t):
                return
            pair, half = divmod(t, 2)
            if half == 0:
                y_sb[pair] = stream3.tile([P, 2, C], F32, name="y_sb")
            nc.vector.tensor_tensor(out=y_sb[pair][:, half, :], in0=y_acc.pop(t)[:], in1=bo_rows[:], op=ALU.add)
            if pair == ALL_TILES // 2 - 1:
                nc.sync.dma_start(out=out.flatten_outer_dims()[t * P : (t + 1) * P, :], in_=y_sb[pair][:, half, :])
            elif half == 1:
                rows = out.flatten_outer_dims()[pair * 2 * P : (pair + 1) * 2 * P, :]
                nc.sync.dma_start(out=rows.rearrange("(i p) c -> p i c", p=P), in_=y_sb.pop(pair)[:])

        def of_group(step, lag):
            g, i = divmod(step - lag, TILES_PER_GROUP)
            return g if i == 0 and 0 <= g < GROUPS else None

        in_order = {mybir.EngineType.PE, mybir.EngineType.Activation, mybir.EngineType.DVE, mybir.EngineType.Pool}
        stack.enter_context(tc.manual_schedule(engines=in_order))

        for s in range(-16, ALL_TILES + 14):
            make_factor(s - 8)
            if s % 2 == 0:
                transpose_q(s)
                transpose_q(s + 1)
            rows_group = of_group(s, 7)
            if rows_group is not None:
                transpose_factors(rows_group)
            project_q(s + 5)
            project_out(s - 12)

            add_bq(s + 4)
            if rows_group is not None:
                copy_factors(rows_group)
            sum_squares(s)
            root(s)
            for v in range(2):
                g = of_group(s, 8 + v)
                if g is not None:
                    scale_vector(g, v)

            gate(s - 9)
            add_bo_and_store(s - 13)
            factor_pieces(s - 2, 2)
            factor_pieces(s - 1, 0)
            quantise_g(s - 10)
            factor_pieces(s - 1, 1)
            for g in range(VECTOR_GROUPS):
                if s == 2 * g - 7:
                    for i in range(TILES_PER_GROUP):
                        regroup_x(TILES_PER_GROUP * g + i)
                    if g == 0:
                        permute_weight()
                    quantise_x(TILES_PER_GROUP * g)
                    quantise_x(TILES_PER_GROUP * g + 2)
            if s + 10 >= VECTOR_GROUPS * TILES_PER_GROUP:
                quantise_x(s + 10)

            if s + 13 >= VECTOR_GROUPS * TILES_PER_GROUP:
                regroup_x(s + 13)
